import numpy as np
import ml_dtypes


def mxq(x, axis, fmt="e4m3"):
    dtype, down = {"e4m3": (ml_dtypes.float8_e4m3fn, 7), "e5m2": (ml_dtypes.float8_e5m2, 14)}[fmt]
    v = np.moveaxis(np.asarray(x, np.float32).astype(ml_dtypes.bfloat16).astype(np.float64), axis, -1)
    blocks = v.reshape(v.shape[:-1] + (-1, 32))
    amax = np.abs(blocks).max(-1, keepdims=True)
    byte = np.maximum(np.where(amax > 0, np.frexp(amax)[1] - 1 + 127, 0) - down, 1)
    scale = np.exp2(byte - 127.0)
    codes = (blocks / scale).astype(np.float32).astype(dtype).astype(np.float64)
    return np.moveaxis((codes * scale).reshape(v.shape), -1, axis)


WIDE = False


def mx_kscale(k):
    if not WIDE:
        return np.ones(k)
    levels = np.array([10, -10, 5, -5, 0])
    a = np.random.permutation(np.resize(levels, k // 512 * 4)).reshape(k // 512, 4)
    idx = np.arange(k)
    return np.exp2(a[idx // 512, idx % 128 // 32])


BF16 = ml_dtypes.bfloat16


def bf(x):
    return np.asarray(x, np.float32).astype(BF16)


def f64(x):
    return np.asarray(x).astype(np.float64)


E2M1 = np.array([0.0, 0.5, 1.0, 1.5, 2.0, 3.0, 4.0, 6.0, -0.0, -0.5, -1.0, -1.5, -2.0, -3.0, -4.0, -6.0])


def pack_weight(w, fmt):
    k, n = w.shape
    w = f64(bf(w)).reshape(k // 32, 32, n)
    amax = np.abs(w).max(1)
    if fmt == "e4m3":
        byte = np.frexp(amax)[1] - 1 + 127 - 7
    else:
        mant, ex = np.frexp(amax / 6.0)
        byte = np.where(mant > 0.5, ex, ex - 1) + 127
    byte = np.clip(np.where(amax > 0, byte, 1), 1, 254)
    scaled = (w * np.exp2(127.0 - byte)[:, None, :]).reshape(k, n).astype(np.float32)
    by_word = np.ascontiguousarray(scaled.reshape(k // 512, 128, 4, n).transpose(0, 1, 3, 2))
    if fmt == "e4m3":
        words = by_word.astype(ml_dtypes.float8_e4m3fn).view(np.uint8)
    else:
        c = by_word.astype(ml_dtypes.float4_e2m1fn).view(np.uint8) & 0xF
        words = c[..., 0::2] | (c[..., 1::2] << 4)
    return np.ascontiguousarray(words), np.ascontiguousarray(byte.astype(np.uint8).reshape(k // 512, 16, n))


def unpack_weight(words, scales, fmt):
    g, p, n, _ = words.shape
    if fmt == "e4m3":
        vals = np.ascontiguousarray(words).view(ml_dtypes.float8_e4m3fn).astype(np.float64)
    else:
        nib = np.empty((g, p, n, 4), np.uint8)
        nib[..., 0::2] = words & 0xF
        nib[..., 1::2] = words >> 4
        vals = E2M1[nib]
    vals = vals * np.repeat(np.exp2(scales.astype(np.float64) - 127.0), 8, axis=1)[..., None]
    return vals.transpose(0, 1, 3, 2).reshape(g * 512, n)


B, In, H, Hh, E, G = 256, 8192, 8192, 256, 128, 4
K = In + H
EPS = 1e-6
FMT = "e4m3"


def rn(*shape):
    return np.random.standard_normal(shape)


def sigmoid(v):
    return 1.0 / (1.0 + np.exp(-v))


def ln(a, gamma, beta):
    mean = a.mean(-1, keepdims=True)
    std = a.std(-1, keepdims=True, ddof=1)
    return gamma * (a - mean) / (std + EPS) + beta


def setup_inputs():
    s = mx_kscale(K)
    x = bf(rn(B, In) * s[:In])
    h = bf(rn(B, H) * s[In:])
    hyper_h = bf(rn(B, Hh))
    hyper_c = bf(rn(B, Hh))
    wih = rn(G * Hh, K) / np.sqrt(K) / s[None, :]
    hc_Wih_words, hc_Wih_scales = pack_weight(np.ascontiguousarray(wih.T), FMT)
    return {
        'x': x,
        'h': h,
        'hyper_h': hyper_h,
        'hyper_c': hyper_c,
        'hc_Wih_words': hc_Wih_words,
        'hc_Wih_scales': hc_Wih_scales,
        'hc_bih': bf(0.3 * rn(G * Hh)),
        'hc_Whh': bf(rn(G * Hh, Hh) / np.sqrt(Hh)),
        'hc_ln_gamma': bf(1.0 + 0.1 * rn(G, Hh)),
        'hc_ln_beta': bf(0.1 * rn(G, Hh)),
        'hc_lnc_gamma': bf(1.0 + 0.1 * rn(Hh)),
        'hc_lnc_beta': bf(0.1 * rn(Hh)),
    }


def reference(x, h, hyper_h, hyper_c, hc_Wih_words, hc_Wih_scales, hc_bih, hc_Whh, hc_ln_gamma, hc_ln_beta, hc_lnc_gamma, hc_lnc_beta):
    hyper_in = np.concatenate([f64(x), f64(h)], axis=1)
    v = (mxq(hyper_in, 1, 'e4m3') @ unpack_weight(hc_Wih_words, hc_Wih_scales, FMT)) + f64(hc_bih) + f64(hyper_h) @ f64(hc_Whh).T
    v = ln(v.reshape(B, G, Hh), f64(hc_ln_gamma), f64(hc_ln_beta))
    hi, hf, hg, ho = v[:, 0], v[:, 1], v[:, 2], v[:, 3]
    hf = hf + 1.0
    new_hyper_c = f64(hyper_c) * sigmoid(hf) + sigmoid(hi) * np.tanh(hg)
    new_hyper_c = ln(new_hyper_c, f64(hc_lnc_gamma), f64(hc_lnc_beta))
    new_hyper_h = np.tanh(new_hyper_c) * sigmoid(ho)
    return new_hyper_h, new_hyper_c

@@ -1,0 +1,312 @@
+import math
+from contextlib import ExitStack
+
+import concourse.mybir as mybir
+from concourse.masks import make_identity
+
+F32 = mybir.dt.float32
+BF16 = mybir.dt.bfloat16
+I32 = mybir.dt.int32
+U32 = mybir.dt.uint32
+U8 = mybir.dt.uint8
+FP8X4 = mybir.dt.float8_e4m3fn_x4
+ALU = mybir.AluOpType
+ACT = mybir.ActivationFunctionType
+
+P = 128
+BATCH = 256
+M_TILES = BATCH // P
+IN = 8192
+K = 2 * IN
+K_PASS = 4 * P
+GROUPS = K // K_PASS
+UNITS = 256
+GATES = 4
+N = GATES * UNITS
+N_IFG = 3 * UNITS
+BANK = 512
+EPS = 1e-6
+
+U_CHUNK = 4
+W_CHUNK = 4
+PLANES = 4
+PLANE_GROUPS = GROUPS // PLANES
+
+ROW_BIAS = 0
+ROW_GAMMA = 2
+ROW_BETA = 4
+ROW_CELL = 6
+
+FLOPS = 2 * BATCH * K * N + 2 * BATCH * UNITS * N
+
+
+def tile_hyperlstmcell_pa_k_kernel(
+    tc,
+    x,
+    h,
+    hyper_h,
+    hyper_c,
+    hc_Wih_words,
+    hc_Wih_scales,
+    hc_bih,
+    hc_Whh,
+    hc_ln_gamma,
+    hc_ln_beta,
+    hc_lnc_gamma,
+    hc_lnc_beta,
+    out_0,
+    out_1,
+):
+    nc = tc.nc
+    with ExitStack() as ctx:
+        keep = ctx.enter_context(tc.tile_pool(name="keep", bufs=1))
+        stage = ctx.enter_context(tc.tile_pool(name="stage", bufs=4))
+        wpool = ctx.enter_context(tc.tile_pool(name="wpool", bufs=4))
+        psum = ctx.enter_context(tc.psum_pool(name="psum", bufs=8))
+        ctx.enter_context(tc.manual_schedule())
+
+        vec = keep.tile([P, BANK], BF16)
+        nc.vector.memset(vec[:], 0.0)
+        w_planes = keep.tile([P, PLANE_GROUPS, N], U8, align_bytes=64)
+        nc.vector.memset(w_planes[:].bitcast(I32), 0)
+        half = keep.tile([P, 8], F32)
+        nc.vector.memset(half[:], 0.5)
+        ident_bf = keep.tile([P, P], BF16)
+        make_identity(nc, ident_bf[:])
+        ident_f32 = keep.tile([P, P], F32)
+        make_identity(nc, ident_f32[:])
+
+        hh_sb = keep.tile([P, M_TILES, UNITS], BF16)
+        nc.sync.dma_start(out=hh_sb[:], in_=hyper_h.rearrange("(p m) k -> p m k", m=M_TILES))
+        whh_sb = keep.tile([P, N // P, UNITS], BF16)
+        nc.sync.dma_start(out=whh_sb[:], in_=hc_Whh.rearrange("(p a) k -> p a k", a=N // P))
+        nc.scalar.dma_start(out=vec[ROW_BIAS : ROW_BIAS + 2, :], in_=hc_bih.rearrange("(a n) -> a n", a=2))
+        nc.scalar.dma_start(
+            out=vec[ROW_GAMMA : ROW_GAMMA + 2, :], in_=hc_ln_gamma.rearrange("(a b) n -> a (b n)", a=2)
+        )
+        nc.scalar.dma_start(
+            out=vec[ROW_BETA : ROW_BETA + 2, :], in_=hc_ln_beta.rearrange("(a b) n -> a (b n)", a=2)
+        )
+        nc.scalar.dma_start(out=vec[ROW_CELL : ROW_CELL + 1, 0:UNITS], in_=hc_lnc_gamma.rearrange("(o n) -> o n", o=1))
+        nc.scalar.dma_start(
+            out=vec[ROW_CELL : ROW_CELL + 1, UNITS : 2 * UNITS], in_=hc_lnc_beta.rearrange("(o n) -> o n", o=1)
+        )
+        hc_sb = keep.tile([P, M_TILES, UNITS], BF16)
+        nc.scalar.dma_start(out=hc_sb[:], in_=hyper_c.rearrange("(p m) k -> p m k", m=M_TILES))
+
+        scale_rows = hc_Wih_scales.rearrange("(k j) (q r) n -> k r q j n", k=PLANES, r=4)
+        for kq in range(PLANES):
+            for r in range(4):
+                nc.gpsimd.dma_start(
+                    out=w_planes[4 * kq + r : P : 32, :, :].bitcast(F32),
+                    in_=scale_rows[kq, r].bitcast(F32),
+                )
+
+        def row_selector(row):
+            return ident_bf[:, row : row + 1].to_broadcast([P, P])
+
+        hhT_ps = psum.tile([P, M_TILES, 2, P], BF16, tag="bank")
+        for m in range(M_TILES):
+            for kh in range(2):
+                nc.tensor.transpose(hhT_ps[:, m, kh, :], hh_sb[:, m, kh * P : (kh + 1) * P], ident_bf[:])
+        hhT = keep.tile([P, M_TILES, 2, P], BF16)
+        nc.vector.tensor_copy(out=hhT[:], in_=hhT_ps[:])
+
+        whhT = keep.tile([P, 2, N], BF16)
+        for kh in range(2):
+            whhT_ps = psum.tile([P, N // P, P], BF16, tag="bank")
+            for a in range(N // P):
+                nc.tensor.transpose(whhT_ps[:, a, :], whh_sb[:, a, kh * P : (kh + 1) * P], ident_bf[:])
+            nc.vector.tensor_copy(
+                out=whhT[:, kh, :].rearrange("k (p a) -> k p a", a=N // P),
+                in_=whhT_ps[:].rearrange("k a p -> k p a"),
+            )
+
+        gamma = keep.tile([P, N], F32)
+        beta = keep.tile([P, N], F32)
+        cell_vec = keep.tile([P, 2 * UNITS], F32)
+        spread = [
+            (ROW_GAMMA, gamma[:, 0:BANK]),
+            (ROW_GAMMA + 1, gamma[:, BANK:N]),
+            (ROW_BETA, beta[:, 0:BANK]),
+            (ROW_BETA + 1, beta[:, BANK:N]),
+            (ROW_CELL, cell_vec[:]),
+        ]
+        for row, dest in spread:
+            spread_ps = psum.tile([P, BANK], F32, tag="bank")
+            nc.tensor.matmul(spread_ps[:], lhsT=row_selector(row), rhs=vec[:], start=True, stop=True)
+            nc.scalar.copy(out=dest, in_=spread_ps[:])
+        nc.vector.tensor_scalar_add(out=beta[:, UNITS : 2 * UNITS], in0=beta[:, UNITS : 2 * UNITS], scalar1=1.0)
+
+        pre = keep.tile([P, M_TILES, N], F32)
+        for m in range(M_TILES):
+            for nh in range(N // BANK):
+                cols = slice(nh * BANK, (nh + 1) * BANK)
+                pre_ps = psum.tile([P, BANK], F32, tag="bank")
+                for kh in range(2):
+                    nc.tensor.matmul(
+                        pre_ps[:], lhsT=hhT[:, m, kh, :], rhs=whhT[:, kh, cols], start=(kh == 0), stop=False
+                    )
+                nc.tensor.matmul(pre_ps[:], lhsT=row_selector(ROW_BIAS + nh), rhs=vec[:], start=False, stop=True)
+                nc.scalar.copy(out=pre[:, m, cols], in_=pre_ps[:])
+
+        u_codes = keep.tile([P, GROUPS, BATCH], U32, align_bytes=64)
+        u_planes = keep.tile([P, GROUPS, BATCH], U8, align_bytes=64)
+        grouped_tiles = []
+
+        def quantise(g):
+            nc.vector.quantize_mx(
+                out=u_codes[:, g, :].bitcast(FP8X4), scales=u_planes[:, g, :], in_=grouped_tiles[g][:]
+            )
+
+        for g in range(GROUPS):
+            if g % U_CHUNK == 0:
+                source = x if g < GROUPS // 2 else h
+                k0 = (g % (GROUPS // 2)) * K_PASS
+                u_sb = stage.tile([P, M_TILES, U_CHUNK * K_PASS], BF16)
+                nc.sync.dma_start(
+                    out=u_sb[:],
+                    in_=source.rearrange("(p m) k -> p m k", m=M_TILES)[:, :, k0 : k0 + U_CHUNK * K_PASS],
+                )
+            first_word = (g % U_CHUNK) * (K_PASS // 2)
+            uT_ps = psum.tile([P, M_TILES, 2, P], F32, tag="bank")
+            for m in range(M_TILES):
+                words = u_sb[:, m, :].bitcast(F32)
+                for w in range(2):
+                    nc.tensor.transpose(
+                        uT_ps[:, m, w, :], words[:, first_word + w : first_word + K_PASS // 2 : 2], ident_f32[:]
+                    )
+            grouped = stage.tile([P, 4 * BATCH], BF16, align_bytes=64)
+            grouped_tiles.append(grouped)
+            copy = nc.vector.tensor_copy if g % 4 == 3 else nc.scalar.copy
+            copy(
+                out=grouped[:].bitcast(F32).rearrange("p (m r w) -> p m r w", m=M_TILES, w=2),
+                in_=uT_ps[:].rearrange("p m w r -> p m r w"),
+            )
+            if g > 0:
+                quantise(g - 1)
+        quantise(GROUPS - 1)
+
+        def mx_pass(acc, g, m, w_words, n_cols):
+            kq, j = divmod(g, PLANE_GROUPS)
+            rows = slice(m * P, (m + 1) * P)
+            nc.tensor.matmul_mx(
+                out=acc,
+                lhsT=u_codes[:, g, rows].bitcast(FP8X4),
+                lhsT_scale=u_planes[:, g, rows],
+                rhs=w_words.bitcast(FP8X4),
+                rhs_scale=w_planes[4 * kq : P, j, n_cols],
+                start=(g == 0),
+                stop=(g == GROUPS - 1),
+            )
+
+        w_bytes = hc_Wih_words.rearrange("g p n t -> p g (n t)")
+        acc_if = [psum.tile([P, 2 * UNITS], F32, tag="bank", name="acc_if%d" % m) for m in range(M_TILES)]
+        acc_g = [psum.tile([P, UNITS], F32, tag="bank", name="acc_g%d" % m) for m in range(M_TILES)]
+        acc_o = [psum.tile([P, UNITS], F32, tag="bank", name="acc_o%d" % m) for m in range(M_TILES)]
+
+        for g0 in range(0, GROUPS, W_CHUNK):
+            w_ifg = wpool.tile([P, W_CHUNK, N_IFG], U32, align_bytes=64)
+            nc.sync.dma_start(
+                out=w_ifg[:].bitcast(I32), in_=w_bytes[:, g0 : g0 + W_CHUNK, 0 : 4 * N_IFG].bitcast(I32)
+            )
+            for gl in range(W_CHUNK):
+                for m in range(M_TILES):
+                    mx_pass(acc_if[m][:], g0 + gl, m, w_ifg[:, gl, 0 : 2 * UNITS], slice(0, 2 * UNITS))
+                    mx_pass(acc_g[m][:], g0 + gl, m, w_ifg[:, gl, 2 * UNITS : N_IFG], slice(2 * UNITS, N_IFG))
+
+        w_o_tiles = []
+        for g0 in range(0, GROUPS, W_CHUNK):
+            w_o = wpool.tile([P, W_CHUNK, UNITS], U32, align_bytes=64, bufs=GROUPS // W_CHUNK)
+            nc.sync.dma_start(
+                out=w_o[:].bitcast(I32), in_=w_bytes[:, g0 : g0 + W_CHUNK, 4 * N_IFG : 4 * N].bitcast(I32)
+            )
+            w_o_tiles.append(w_o)
+
+        def layer_norm(label, rows):
+            n = len(rows)
+            stats = keep.tile([P, n, 6], F32, name="stats_" + label)
+            mean_var = keep.tile([P, n, 2], F32, name="mean_var_" + label)
+            std = keep.tile([P, n], F32, name="std_" + label)
+            rstd = keep.tile([P, n], F32, name="rstd_" + label)
+            for i in range(n):
+                nc.vector.bn_stats(out=stats[:, i, :], in_=rows[i][0])
+            for i in range(n):
+                nc.vector.bn_aggr(out=mean_var[:, i, :], in_=stats[:, i, :])
+            nc.gpsimd.tensor_tensor(out=std[:], in0=mean_var[:, :, 1], in1=half[:, 0:n], op=ALU.pow)
+            for i in range(n):
+                nc.vector.scalar_tensor_tensor(
+                    out=rows[i][0], in0=rows[i][0], scalar=mean_var[:, i, 0:1], in1=rows[i][1],
+                    op0=ALU.subtract, op1=ALU.mult,
+                )
+            nc.vector.tensor_scalar(
+                out=std[:], in0=std[:], scalar1=math.sqrt(UNITS / (UNITS - 1)), scalar2=EPS,
+                op0=ALU.mult, op1=ALU.add,
+            )
+            nc.vector.reciprocal(out=rstd[:], in_=std[:])
+            for i in range(n):
+                nc.vector.scalar_tensor_tensor(
+                    out=rows[i][0], in0=rows[i][0], scalar=rstd[:, i : i + 1], in1=rows[i][2],
+                    op0=ALU.mult, op1=ALU.add,
+                )
+
+        def gate_cols(gate):
+            return slice(gate * UNITS, (gate + 1) * UNITS)
+
+        v = keep.tile([P, M_TILES, N], F32)
+        act = keep.tile([P, M_TILES, N], F32)
+        cell = keep.tile([P, M_TILES, UNITS], F32)
+        in_part = keep.tile([P, M_TILES, UNITS], F32)
+        tanh_cell = keep.tile([P, M_TILES, UNITS], F32)
+        hidden = keep.tile([P, M_TILES, UNITS], F32)
+
+        for m in range(M_TILES):
+            nc.vector.tensor_tensor(
+                out=v[:, m, 0 : 2 * UNITS], in0=acc_if[m][:], in1=pre[:, m, 0 : 2 * UNITS], op=ALU.add
+            )
+            nc.vector.tensor_tensor(
+                out=v[:, m, gate_cols(2)], in0=acc_g[m][:], in1=pre[:, m, gate_cols(2)], op=ALU.add
+            )
+        layer_norm(
+            "ifg",
+            [
+                (v[:, m, gate_cols(q)], gamma[:, gate_cols(q)], beta[:, gate_cols(q)])
+                for m in range(M_TILES)
+                for q in range(3)
+            ],
+        )
+        for m in range(M_TILES):
+            nc.scalar.activation(out=act[:, m, 0 : 2 * UNITS], in_=v[:, m, 0 : 2 * UNITS], func=ACT.Sigmoid)
+            nc.scalar.activation(out=act[:, m, gate_cols(2)], in_=v[:, m, gate_cols(2)], func=ACT.Tanh)
+        for m in range(M_TILES):
+            nc.vector.tensor_tensor(out=cell[:, m, :], in0=act[:, m, gate_cols(1)], in1=hc_sb[:, m, :], op=ALU.mult)
+            nc.vector.tensor_tensor(
+                out=in_part[:, m, :], in0=act[:, m, gate_cols(0)], in1=act[:, m, gate_cols(2)], op=ALU.mult
+            )
+        for m in range(M_TILES):
+            nc.vector.tensor_tensor(out=cell[:, m, :], in0=cell[:, m, :], in1=in_part[:, m, :], op=ALU.add)
+        layer_norm(
+            "cell",
+            [(cell[:, m, :], cell_vec[:, 0:UNITS], cell_vec[:, UNITS : 2 * UNITS]) for m in range(M_TILES)],
+        )
+        nc.sync.dma_start(out=out_1.rearrange("(p m) c -> p m c", m=M_TILES), in_=cell[:])
+        for m in range(M_TILES):
+            nc.scalar.activation(out=tanh_cell[:, m, :], in_=cell[:, m, :], func=ACT.Tanh)
+
+        for c in range(GROUPS // W_CHUNK):
+            for gl in range(W_CHUNK):
+                for m in range(M_TILES):
+                    mx_pass(acc_o[m][:], c * W_CHUNK + gl, m, w_o_tiles[c][:, gl, :], gate_cols(3))
+        for m in range(M_TILES):
+            nc.vector.tensor_tensor(
+                out=v[:, m, gate_cols(3)], in0=acc_o[m][:], in1=pre[:, m, gate_cols(3)], op=ALU.add
+            )
+        layer_norm(
+            "o", [(v[:, m, gate_cols(3)], gamma[:, gate_cols(3)], beta[:, gate_cols(3)]) for m in range(M_TILES)]
+        )
+        for m in range(M_TILES):
+            nc.scalar.activation(out=act[:, m, gate_cols(3)], in_=v[:, m, gate_cols(3)], func=ACT.Sigmoid)
+            nc.vector.tensor_tensor(
+                out=hidden[:, m, :], in0=tanh_cell[:, m, :], in1=act[:, m, gate_cols(3)], op=ALU.mult
+            )
+        nc.sync.dma_start(out=out_0.rearrange("(p m) c -> p m c", m=M_TILES), in_=hidden[:])

@@ -29,8 +29,8 @@ EPS = 1e-6
 
 U_CHUNK = 4
 W_CHUNK = 4
-PLANES = 4
-PLANE_GROUPS = GROUPS // PLANES
+OFFSETS = 4
+OFFSET_GROUPS = GROUPS // OFFSETS
 
 ROW_BIAS = 0
 ROW_GAMMA = 2
@@ -67,8 +67,9 @@ def tile_hyperlstmcell_pa_k_kernel(
 
         vec = keep.tile([P, BANK], BF16)
         nc.vector.memset(vec[:], 0.0)
-        w_planes = keep.tile([P, PLANE_GROUPS, N], U8, align_bytes=64)
-        nc.vector.memset(w_planes[:].bitcast(I32), 0)
+        w_planes = keep.tile([P, GROUPS, N], U8, align_bytes=64)
+        for kq in range(OFFSETS):
+            nc.vector.memset(w_planes[:, kq * OFFSET_GROUPS : (kq + 1) * OFFSET_GROUPS, :].bitcast(I32), 0)
         half = keep.tile([P, 8], F32)
         nc.vector.memset(half[:], 0.5)
         ident_bf = keep.tile([P, P], BF16)
@@ -94,11 +95,11 @@ def tile_hyperlstmcell_pa_k_kernel(
         hc_sb = keep.tile([P, M_TILES, UNITS], BF16)
         nc.scalar.dma_start(out=hc_sb[:], in_=hyper_c.rearrange("(p m) k -> p m k", m=M_TILES))
 
-        scale_rows = hc_Wih_scales.rearrange("(k j) (q r) n -> k r q j n", k=PLANES, r=4)
-        for kq in range(PLANES):
+        scale_rows = hc_Wih_scales.rearrange("(k j) (q r) n -> k r q j n", k=OFFSETS, r=4)
+        for kq in range(OFFSETS):
             for r in range(4):
                 nc.gpsimd.dma_start(
-                    out=w_planes[4 * kq + r : P : 32, :, :].bitcast(F32),
+                    out=w_planes[4 * kq + r : P : 32, kq * OFFSET_GROUPS : (kq + 1) * OFFSET_GROUPS, :].bitcast(F32),
                     in_=scale_rows[kq, r].bitcast(F32),
                 )
 
@@ -138,7 +139,7 @@ def tile_hyperlstmcell_pa_k_kernel(
             nc.scalar.copy(out=dest, in_=spread_ps[:])
         nc.vector.tensor_scalar_add(out=beta[:, UNITS : 2 * UNITS], in0=beta[:, UNITS : 2 * UNITS], scalar1=1.0)
 
-        pre = keep.tile([P, M_TILES, N], F32)
+        v = keep.tile([P, M_TILES, N], F32)
         for m in range(M_TILES):
             for nh in range(N // BANK):
                 cols = slice(nh * BANK, (nh + 1) * BANK)
@@ -148,7 +149,7 @@ def tile_hyperlstmcell_pa_k_kernel(
                         pre_ps[:], lhsT=hhT[:, m, kh, :], rhs=whhT[:, kh, cols], start=(kh == 0), stop=False
                     )
                 nc.tensor.matmul(pre_ps[:], lhsT=row_selector(ROW_BIAS + nh), rhs=vec[:], start=False, stop=True)
-                nc.scalar.copy(out=pre[:, m, cols], in_=pre_ps[:])
+                nc.scalar.copy(out=v[:, m, cols], in_=pre_ps[:])
 
         u_codes = keep.tile([P, GROUPS, BATCH], U32, align_bytes=64)
         u_planes = keep.tile([P, GROUPS, BATCH], U8, align_bytes=64)
@@ -188,14 +189,14 @@ def tile_hyperlstmcell_pa_k_kernel(
         quantise(GROUPS - 1)
 
         def mx_pass(acc, g, m, w_words, n_cols):
-            kq, j = divmod(g, PLANE_GROUPS)
+            kq = g // OFFSET_GROUPS
             rows = slice(m * P, (m + 1) * P)
             nc.tensor.matmul_mx(
                 out=acc,
                 lhsT=u_codes[:, g, rows].bitcast(FP8X4),
                 lhsT_scale=u_planes[:, g, rows],
                 rhs=w_words.bitcast(FP8X4),
-                rhs_scale=w_planes[4 * kq : P, j, n_cols],
+                rhs_scale=w_planes[4 * kq : P, g, n_cols],
                 start=(g == 0),
                 stop=(g == GROUPS - 1),
             )
@@ -253,19 +254,16 @@ def tile_hyperlstmcell_pa_k_kernel(
         def gate_cols(gate):
             return slice(gate * UNITS, (gate + 1) * UNITS)
 
-        v = keep.tile([P, M_TILES, N], F32)
-        act = keep.tile([P, M_TILES, N], F32)
         cell = keep.tile([P, M_TILES, UNITS], F32)
         in_part = keep.tile([P, M_TILES, UNITS], F32)
-        tanh_cell = keep.tile([P, M_TILES, UNITS], F32)
         hidden = keep.tile([P, M_TILES, UNITS], F32)
 
         for m in range(M_TILES):
             nc.vector.tensor_tensor(
-                out=v[:, m, 0 : 2 * UNITS], in0=acc_if[m][:], in1=pre[:, m, 0 : 2 * UNITS], op=ALU.add
+                out=v[:, m, 0 : 2 * UNITS], in0=acc_if[m][:], in1=v[:, m, 0 : 2 * UNITS], op=ALU.add
             )
             nc.vector.tensor_tensor(
-                out=v[:, m, gate_cols(2)], in0=acc_g[m][:], in1=pre[:, m, gate_cols(2)], op=ALU.add
+                out=v[:, m, gate_cols(2)], in0=acc_g[m][:], in1=v[:, m, gate_cols(2)], op=ALU.add
             )
         layer_norm(
             "ifg",
@@ -276,12 +274,12 @@ def tile_hyperlstmcell_pa_k_kernel(
             ],
         )
         for m in range(M_TILES):
-            nc.scalar.activation(out=act[:, m, 0 : 2 * UNITS], in_=v[:, m, 0 : 2 * UNITS], func=ACT.Sigmoid)
-            nc.scalar.activation(out=act[:, m, gate_cols(2)], in_=v[:, m, gate_cols(2)], func=ACT.Tanh)
+            nc.scalar.activation(out=v[:, m, 0 : 2 * UNITS], in_=v[:, m, 0 : 2 * UNITS], func=ACT.Sigmoid)
+            nc.scalar.activation(out=v[:, m, gate_cols(2)], in_=v[:, m, gate_cols(2)], func=ACT.Tanh)
         for m in range(M_TILES):
-            nc.vector.tensor_tensor(out=cell[:, m, :], in0=act[:, m, gate_cols(1)], in1=hc_sb[:, m, :], op=ALU.mult)
+            nc.vector.tensor_tensor(out=cell[:, m, :], in0=v[:, m, gate_cols(1)], in1=hc_sb[:, m, :], op=ALU.mult)
             nc.vector.tensor_tensor(
-                out=in_part[:, m, :], in0=act[:, m, gate_cols(0)], in1=act[:, m, gate_cols(2)], op=ALU.mult
+                out=in_part[:, m, :], in0=v[:, m, gate_cols(0)], in1=v[:, m, gate_cols(2)], op=ALU.mult
             )
         for m in range(M_TILES):
             nc.vector.tensor_tensor(out=cell[:, m, :], in0=cell[:, m, :], in1=in_part[:, m, :], op=ALU.add)
@@ -291,7 +289,7 @@ def tile_hyperlstmcell_pa_k_kernel(
         )
         nc.sync.dma_start(out=out_1.rearrange("(p m) c -> p m c", m=M_TILES), in_=cell[:])
         for m in range(M_TILES):
-            nc.scalar.activation(out=tanh_cell[:, m, :], in_=cell[:, m, :], func=ACT.Tanh)
+            nc.scalar.activation(out=hidden[:, m, :], in_=cell[:, m, :], func=ACT.Tanh)
 
         for c in range(GROUPS // W_CHUNK):
             for gl in range(W_CHUNK):
@@ -299,14 +297,14 @@ def tile_hyperlstmcell_pa_k_kernel(
                     mx_pass(acc_o[m][:], c * W_CHUNK + gl, m, w_o_tiles[c][:, gl, :], gate_cols(3))
         for m in range(M_TILES):
             nc.vector.tensor_tensor(
-                out=v[:, m, gate_cols(3)], in0=acc_o[m][:], in1=pre[:, m, gate_cols(3)], op=ALU.add
+                out=v[:, m, gate_cols(3)], in0=acc_o[m][:], in1=v[:, m, gate_cols(3)], op=ALU.add
             )
         layer_norm(
             "o", [(v[:, m, gate_cols(3)], gamma[:, gate_cols(3)], beta[:, gate_cols(3)]) for m in range(M_TILES)]
         )
         for m in range(M_TILES):
-            nc.scalar.activation(out=act[:, m, gate_cols(3)], in_=v[:, m, gate_cols(3)], func=ACT.Sigmoid)
+            nc.scalar.activation(out=v[:, m, gate_cols(3)], in_=v[:, m, gate_cols(3)], func=ACT.Sigmoid)
             nc.vector.tensor_tensor(
-                out=hidden[:, m, :], in0=tanh_cell[:, m, :], in1=act[:, m, gate_cols(3)], op=ALU.mult
+                out=hidden[:, m, :], in0=hidden[:, m, :], in1=v[:, m, gate_cols(3)], op=ALU.mult
             )
         nc.sync.dma_start(out=out_0.rearrange("(p m) c -> p m c", m=M_TILES), in_=hidden[:])

@@ -67,9 +67,8 @@ def tile_hyperlstmcell_pa_k_kernel(
 
         vec = keep.tile([P, BANK], BF16)
         nc.vector.memset(vec[:], 0.0)
-        w_planes = keep.tile([P, GROUPS, N], U8, align_bytes=64)
-        for kq in range(OFFSETS):
-            nc.vector.memset(w_planes[:, kq * OFFSET_GROUPS : (kq + 1) * OFFSET_GROUPS, :].bitcast(I32), 0)
+        w_planes = keep.tile([P, OFFSET_GROUPS, N], U8, align_bytes=64)
+        nc.vector.memset(w_planes[:].bitcast(I32), 0)
         half = keep.tile([P, 8], F32)
         nc.vector.memset(half[:], 0.5)
         ident_bf = keep.tile([P, P], BF16)
@@ -95,13 +94,13 @@ def tile_hyperlstmcell_pa_k_kernel(
         hc_sb = keep.tile([P, M_TILES, UNITS], BF16)
         nc.scalar.dma_start(out=hc_sb[:], in_=hyper_c.rearrange("(p m) k -> p m k", m=M_TILES))
 
-        scale_rows = hc_Wih_scales.rearrange("(k j) (q r) n -> k r q j n", k=OFFSETS, r=4)
-        for kq in range(OFFSETS):
-            for r in range(4):
-                nc.gpsimd.dma_start(
-                    out=w_planes[4 * kq + r : P : 32, kq * OFFSET_GROUPS : (kq + 1) * OFFSET_GROUPS, :].bitcast(F32),
-                    in_=scale_rows[kq, r].bitcast(F32),
-                )
+        scale_rows = hc_Wih_scales.rearrange("(k j) q n -> q k j n", k=OFFSETS)
+        for q in range(16):
+            first = 32 * (q // 4) + q % 4
+            nc.sync.dma_start(
+                out=w_planes[first : first + 4 * OFFSETS : 4, :, :].bitcast(I32),
+                in_=scale_rows[q].bitcast(I32),
+            )
 
         def row_selector(row):
             return ident_bf[:, row : row + 1].to_broadcast([P, P])
@@ -189,14 +188,14 @@ def tile_hyperlstmcell_pa_k_kernel(
         quantise(GROUPS - 1)
 
         def mx_pass(acc, g, m, w_words, n_cols):
-            kq = g // OFFSET_GROUPS
+            kq, j = divmod(g, OFFSET_GROUPS)
             rows = slice(m * P, (m + 1) * P)
             nc.tensor.matmul_mx(
                 out=acc,
                 lhsT=u_codes[:, g, rows].bitcast(FP8X4),
                 lhsT_scale=u_planes[:, g, rows],
                 rhs=w_words.bitcast(FP8X4),
-                rhs_scale=w_planes[4 * kq : P, g, n_cols],
+                rhs_scale=w_planes[4 * kq : P, j, n_cols],
                 start=(g == 0),
                 stop=(g == GROUPS - 1),
             )

@@ -29,8 +29,8 @@ EPS = 1e-6
 
 U_CHUNK = 4
 W_CHUNK = 4
-OFFSETS = 4
-OFFSET_GROUPS = GROUPS // OFFSETS
+SCALE_SETS = 4
+SET_GROUPS = GROUPS // SCALE_SETS
 
 ROW_BIAS = 0
 ROW_GAMMA = 2
@@ -67,8 +67,16 @@ def tile_hyperlstmcell_pa_k_kernel(
 
         vec = keep.tile([P, BANK], BF16)
         nc.vector.memset(vec[:], 0.0)
-        w_planes = keep.tile([P, OFFSET_GROUPS, N], U8, align_bytes=64)
-        nc.vector.memset(w_planes[:].bitcast(I32), 0)
+        w_planes = keep.tile([P, GROUPS, N], U8, align_bytes=64)
+        scale_rows = hc_Wih_scales.rearrange("(s j) (q r) n -> s r q j n", s=SCALE_SETS, r=4)
+
+        def zero_planes(s):
+            nc.vector.memset(w_planes[:, s * SET_GROUPS : (s + 1) * SET_GROUPS, :].bitcast(I32), 0)
+
+        def plane_rows(s, r):
+            return w_planes[r : P : 32, s * SET_GROUPS : (s + 1) * SET_GROUPS, :]
+
+        zero_planes(0)
         half = keep.tile([P, 8], F32)
         nc.vector.memset(half[:], 0.5)
         ident_bf = keep.tile([P, P], BF16)
@@ -94,13 +102,8 @@ def tile_hyperlstmcell_pa_k_kernel(
         hc_sb = keep.tile([P, M_TILES, UNITS], BF16)
         nc.scalar.dma_start(out=hc_sb[:], in_=hyper_c.rearrange("(p m) k -> p m k", m=M_TILES))
 
-        scale_rows = hc_Wih_scales.rearrange("(k j) q n -> q k j n", k=OFFSETS)
-        for q in range(16):
-            first = 32 * (q // 4) + q % 4
-            nc.sync.dma_start(
-                out=w_planes[first : first + 4 * OFFSETS : 4, :, :].bitcast(I32),
-                in_=scale_rows[q].bitcast(I32),
-            )
+        for r in range(4):
+            nc.sync.dma_start(out=plane_rows(0, r).bitcast(I32), in_=scale_rows[0, r].bitcast(I32))
 
         def row_selector(row):
             return ident_bf[:, row : row + 1].to_broadcast([P, P])
@@ -187,15 +190,19 @@ def tile_hyperlstmcell_pa_k_kernel(
                 quantise(g - 1)
         quantise(GROUPS - 1)
 
+        for s in range(1, SCALE_SETS):
+            zero_planes(s)
+            for r in range(4):
+                nc.gpsimd.dma_start(out=plane_rows(s, r).bitcast(F32), in_=scale_rows[s, r].bitcast(F32))
+
         def mx_pass(acc, g, m, w_words, n_cols):
-            kq, j = divmod(g, OFFSET_GROUPS)
             rows = slice(m * P, (m + 1) * P)
             nc.tensor.matmul_mx(
                 out=acc,
                 lhsT=u_codes[:, g, rows].bitcast(FP8X4),
                 lhsT_scale=u_planes[:, g, rows],
                 rhs=w_words.bitcast(FP8X4),
-                rhs_scale=w_planes[4 * kq : P, j, n_cols],
+                rhs_scale=w_planes[:, g, n_cols],
                 start=(g == 0),
                 stop=(g == GROUPS - 1),
             )
@@ -210,8 +217,8 @@ def tile_hyperlstmcell_pa_k_kernel(
             nc.sync.dma_start(
                 out=w_ifg[:].bitcast(I32), in_=w_bytes[:, g0 : g0 + W_CHUNK, 0 : 4 * N_IFG].bitcast(I32)
             )
-            for gl in range(W_CHUNK):
-                for m in range(M_TILES):
+            for m in range(M_TILES):
+                for gl in range(W_CHUNK):
                     mx_pass(acc_if[m][:], g0 + gl, m, w_ifg[:, gl, 0 : 2 * UNITS], slice(0, 2 * UNITS))
                     mx_pass(acc_g[m][:], g0 + gl, m, w_ifg[:, gl, 2 * UNITS : N_IFG], slice(2 * UNITS, N_IFG))
 
@@ -223,87 +230,109 @@ def tile_hyperlstmcell_pa_k_kernel(
             )
             w_o_tiles.append(w_o)
 
-        def layer_norm(label, rows):
-            n = len(rows)
-            stats = keep.tile([P, n, 6], F32, name="stats_" + label)
-            mean_var = keep.tile([P, n, 2], F32, name="mean_var_" + label)
-            std = keep.tile([P, n], F32, name="std_" + label)
-            rstd = keep.tile([P, n], F32, name="rstd_" + label)
-            for i in range(n):
-                nc.vector.bn_stats(out=stats[:, i, :], in_=rows[i][0])
-            for i in range(n):
-                nc.vector.bn_aggr(out=mean_var[:, i, :], in_=stats[:, i, :])
-            nc.gpsimd.tensor_tensor(out=std[:], in0=mean_var[:, :, 1], in1=half[:, 0:n], op=ALU.pow)
-            for i in range(n):
-                nc.vector.scalar_tensor_tensor(
-                    out=rows[i][0], in0=rows[i][0], scalar=mean_var[:, i, 0:1], in1=rows[i][1],
-                    op0=ALU.subtract, op1=ALU.mult,
-                )
-            nc.vector.tensor_scalar(
-                out=std[:], in0=std[:], scalar1=math.sqrt(UNITS / (UNITS - 1)), scalar2=EPS,
-                op0=ALU.mult, op1=ALU.add,
-            )
-            nc.vector.reciprocal(out=rstd[:], in_=std[:])
-            for i in range(n):
-                nc.vector.scalar_tensor_tensor(
-                    out=rows[i][0], in0=rows[i][0], scalar=rstd[:, i : i + 1], in1=rows[i][2],
+        def layer_norm(label, rows_by_tile, squares):
+            n = len(rows_by_tile[0])
+            shape = [P, M_TILES, n]
+            total = keep.tile(shape, F32, name="total_" + label)
+            neg_mean = keep.tile(shape, F32, name="neg_mean_" + label)
+            sq_sum = keep.tile(shape, F32, name="sq_sum_" + label)
+            root = keep.tile(shape, F32, name="root_" + label)
+            rstd = keep.tile(shape, F32, name="rstd_" + label)
+            for m, rows in enumerate(rows_by_tile):
+                for i, row in enumerate(rows):
+                    nc.vector.scalar_tensor_tensor(
+                        out=row["s"], in0=row["first"], scalar=0.0, in1=row["second"],
+                        op0=ALU.add, op1=ALU.add, accum_out=total[:, m, i : i + 1],
+                    )
+                nc.vector.tensor_scalar_mul(out=neg_mean[:, m, :], in0=total[:, m, :], scalar1=-1.0 / UNITS)
+            for m, rows in enumerate(rows_by_tile):
+                for i, row in enumerate(rows):
+                    nc.scalar.activation(
+                        out=squares[:, m, i, :], in_=row["s"], func=ACT.Square,
+                        bias=neg_mean[:, m, i : i + 1], accum_out=sq_sum[:, m, i : i + 1],
+                    )
+                nc.gpsimd.tensor_tensor(out=root[:, m, :], in0=sq_sum[:, m, :], in1=half[:, 0:n], op=ALU.pow)
+            for m, rows in enumerate(rows_by_tile):
+                for i, row in enumerate(rows):
+                    nc.vector.scalar_tensor_tensor(
+                        out=row["out"], in0=row["s"], scalar=neg_mean[:, m, i : i + 1], in1=row["gamma"],
+                        op0=ALU.add, op1=ALU.mult,
+                    )
+            for m, rows in enumerate(rows_by_tile):
+                nc.vector.tensor_scalar(
+                    out=rstd[:, m, :], in0=root[:, m, :], scalar1=1.0 / math.sqrt(UNITS - 1), scalar2=EPS,
                     op0=ALU.mult, op1=ALU.add,
                 )
+                nc.vector.reciprocal(out=rstd[:, m, :], in_=rstd[:, m, :])
+                for i, row in enumerate(rows):
+                    nc.vector.scalar_tensor_tensor(
+                        out=row["out"], in0=row["out"], scalar=rstd[:, m, i : i + 1], in1=row["beta"],
+                        op0=ALU.mult, op1=ALU.add,
+                    )
 
         def gate_cols(gate):
             return slice(gate * UNITS, (gate + 1) * UNITS)
 
-        cell = keep.tile([P, M_TILES, UNITS], F32)
+        def gate_row(m, gate, acc):
+            return dict(
+                first=acc, second=v[:, m, gate_cols(gate)], s=v[:, m, gate_cols(gate)],
+                out=gates[:, m, gate_cols(gate)], gamma=gamma[:, gate_cols(gate)], beta=beta[:, gate_cols(gate)],
+            )
+
+        gates = stage.tile([P, M_TILES, N], F32, tag="u_sb")
+        squares = stage.tile([P, M_TILES, 3, UNITS], F32, tag="u_sb")
+        forget_part = keep.tile([P, M_TILES, UNITS], F32)
         in_part = keep.tile([P, M_TILES, UNITS], F32)
+        cell = keep.tile([P, M_TILES, UNITS], F32)
         hidden = keep.tile([P, M_TILES, UNITS], F32)
 
-        for m in range(M_TILES):
-            nc.vector.tensor_tensor(
-                out=v[:, m, 0 : 2 * UNITS], in0=acc_if[m][:], in1=v[:, m, 0 : 2 * UNITS], op=ALU.add
-            )
-            nc.vector.tensor_tensor(
-                out=v[:, m, gate_cols(2)], in0=acc_g[m][:], in1=v[:, m, gate_cols(2)], op=ALU.add
-            )
         layer_norm(
             "ifg",
             [
-                (v[:, m, gate_cols(q)], gamma[:, gate_cols(q)], beta[:, gate_cols(q)])
+                [
+                    gate_row(m, 0, acc_if[m][:, 0:UNITS]),
+                    gate_row(m, 1, acc_if[m][:, UNITS : 2 * UNITS]),
+                    gate_row(m, 2, acc_g[m][:]),
+                ]
                 for m in range(M_TILES)
-                for q in range(3)
             ],
+            squares,
         )
         for m in range(M_TILES):
-            nc.scalar.activation(out=v[:, m, 0 : 2 * UNITS], in_=v[:, m, 0 : 2 * UNITS], func=ACT.Sigmoid)
-            nc.scalar.activation(out=v[:, m, gate_cols(2)], in_=v[:, m, gate_cols(2)], func=ACT.Tanh)
+            nc.scalar.activation(out=gates[:, m, 0 : 2 * UNITS], in_=gates[:, m, 0 : 2 * UNITS], func=ACT.Sigmoid)
+            nc.scalar.activation(out=gates[:, m, gate_cols(2)], in_=gates[:, m, gate_cols(2)], func=ACT.Tanh)
         for m in range(M_TILES):
-            nc.vector.tensor_tensor(out=cell[:, m, :], in0=v[:, m, gate_cols(1)], in1=hc_sb[:, m, :], op=ALU.mult)
             nc.vector.tensor_tensor(
-                out=in_part[:, m, :], in0=v[:, m, gate_cols(0)], in1=v[:, m, gate_cols(2)], op=ALU.mult
+                out=forget_part[:, m, :], in0=gates[:, m, gate_cols(1)], in1=hc_sb[:, m, :], op=ALU.mult
             )
-        for m in range(M_TILES):
-            nc.vector.tensor_tensor(out=cell[:, m, :], in0=cell[:, m, :], in1=in_part[:, m, :], op=ALU.add)
+            nc.vector.tensor_tensor(
+                out=in_part[:, m, :], in0=gates[:, m, gate_cols(0)], in1=gates[:, m, gate_cols(2)], op=ALU.mult
+            )
         layer_norm(
             "cell",
-            [(cell[:, m, :], cell_vec[:, 0:UNITS], cell_vec[:, UNITS : 2 * UNITS]) for m in range(M_TILES)],
+            [
+                [
+                    dict(
+                        first=forget_part[:, m, :], second=in_part[:, m, :], s=forget_part[:, m, :],
+                        out=cell[:, m, :], gamma=cell_vec[:, 0:UNITS], beta=cell_vec[:, UNITS : 2 * UNITS],
+                    )
+                ]
+                for m in range(M_TILES)
+            ],
+            squares,
         )
         nc.sync.dma_start(out=out_1.rearrange("(p m) c -> p m c", m=M_TILES), in_=cell[:])
         for m in range(M_TILES):
             nc.scalar.activation(out=hidden[:, m, :], in_=cell[:, m, :], func=ACT.Tanh)
 
         for c in range(GROUPS // W_CHUNK):
-            for gl in range(W_CHUNK):
-                for m in range(M_TILES):
+            for m in range(M_TILES):
+                for gl in range(W_CHUNK):
                     mx_pass(acc_o[m][:], c * W_CHUNK + gl, m, w_o_tiles[c][:, gl, :], gate_cols(3))
+        layer_norm("o", [[gate_row(m, 3, acc_o[m][:])] for m in range(M_TILES)], squares)
         for m in range(M_TILES):
+            nc.scalar.activation(out=gates[:, m, gate_cols(3)], in_=gates[:, m, gate_cols(3)], func=ACT.Sigmoid)
             nc.vector.tensor_tensor(
-                out=v[:, m, gate_cols(3)], in0=acc_o[m][:], in1=v[:, m, gate_cols(3)], op=ALU.add
+                out=hidden[:, m, :], in0=hidden[:, m, :], in1=gates[:, m, gate_cols(3)], op=ALU.mult
             )
-        layer_norm(
-            "o", [(v[:, m, gate_cols(3)], gamma[:, gate_cols(3)], beta[:, gate_cols(3)]) for m in range(M_TILES)]
-        )
-        for m in range(M_TILES):
-            nc.scalar.activation(out=v[:, m, gate_cols(3)], in_=v[:, m, gate_cols(3)], func=ACT.Sigmoid)
-            nc.vector.tensor_tensor(
-                out=hidden[:, m, :], in0=hidden[:, m, :], in1=v[:, m, gate_cols(3)], op=ALU.mult
-            )
-        nc.sync.dma_start(out=out_0.rearrange("(p m) c -> p m c", m=M_TILES), in_=hidden[:])
+            nc.sync.dma_start(out=out_0.rearrange("(p m) c -> p m c", m=M_TILES)[:, m, :], in_=hidden[:, m, :])

@@ -29,8 +29,8 @@ EPS = 1e-6
 
 U_CHUNK = 4
 W_CHUNK = 4
-SCALE_SETS = 4
-SET_GROUPS = GROUPS // SCALE_SETS
+OFFSETS = 4
+OFFSET_GROUPS = GROUPS // OFFSETS
 
 ROW_BIAS = 0
 ROW_GAMMA = 2
@@ -67,16 +67,8 @@ def tile_hyperlstmcell_pa_k_kernel(
 
         vec = keep.tile([P, BANK], BF16)
         nc.vector.memset(vec[:], 0.0)
-        w_planes = keep.tile([P, GROUPS, N], U8, align_bytes=64)
-        scale_rows = hc_Wih_scales.rearrange("(s j) (q r) n -> s r q j n", s=SCALE_SETS, r=4)
-
-        def zero_planes(s):
-            nc.vector.memset(w_planes[:, s * SET_GROUPS : (s + 1) * SET_GROUPS, :].bitcast(I32), 0)
-
-        def plane_rows(s, r):
-            return w_planes[r : P : 32, s * SET_GROUPS : (s + 1) * SET_GROUPS, :]
-
-        zero_planes(0)
+        w_planes = keep.tile([P, OFFSET_GROUPS, N], U8, align_bytes=64)
+        nc.vector.memset(w_planes[:].bitcast(I32), 0)
         half = keep.tile([P, 8], F32)
         nc.vector.memset(half[:], 0.5)
         ident_bf = keep.tile([P, P], BF16)
@@ -102,8 +94,13 @@ def tile_hyperlstmcell_pa_k_kernel(
         hc_sb = keep.tile([P, M_TILES, UNITS], BF16)
         nc.scalar.dma_start(out=hc_sb[:], in_=hyper_c.rearrange("(p m) k -> p m k", m=M_TILES))
 
-        for r in range(4):
-            nc.sync.dma_start(out=plane_rows(0, r).bitcast(I32), in_=scale_rows[0, r].bitcast(I32))
+        scale_rows = hc_Wih_scales.rearrange("(k j) q n -> q k j n", k=OFFSETS)
+        for q in range(16):
+            first = 32 * (q // 4) + q % 4
+            nc.sync.dma_start(
+                out=w_planes[first : first + 4 * OFFSETS : 4, :, :].bitcast(I32),
+                in_=scale_rows[q].bitcast(I32),
+            )
 
         def row_selector(row):
             return ident_bf[:, row : row + 1].to_broadcast([P, P])
@@ -190,19 +187,15 @@ def tile_hyperlstmcell_pa_k_kernel(
                 quantise(g - 1)
         quantise(GROUPS - 1)
 
-        for s in range(1, SCALE_SETS):
-            zero_planes(s)
-            for r in range(4):
-                nc.gpsimd.dma_start(out=plane_rows(s, r).bitcast(F32), in_=scale_rows[s, r].bitcast(F32))
-
         def mx_pass(acc, g, m, w_words, n_cols):
+            kq, j = divmod(g, OFFSET_GROUPS)
             rows = slice(m * P, (m + 1) * P)
             nc.tensor.matmul_mx(
                 out=acc,
                 lhsT=u_codes[:, g, rows].bitcast(FP8X4),
                 lhsT_scale=u_planes[:, g, rows],
                 rhs=w_words.bitcast(FP8X4),
-                rhs_scale=w_planes[:, g, n_cols],
+                rhs_scale=w_planes[4 * kq : P, j, n_cols],
                 start=(g == 0),
                 stop=(g == GROUPS - 1),
             )

@@ -28,7 +28,10 @@ BANK = 512
 EPS = 1e-6
 
 U_CHUNK = 4
-W_CHUNK = 4
+U_CHUNKS = GROUPS // U_CHUNK
+W_CHUNK = 2
+O_CHUNK = 4
+T_BANKS = 4
 OFFSETS = 4
 OFFSET_GROUPS = GROUPS // OFFSETS
 
@@ -61,8 +64,8 @@ def tile_hyperlstmcell_pa_k_kernel(
     with ExitStack() as ctx:
         keep = ctx.enter_context(tc.tile_pool(name="keep", bufs=1))
         stage = ctx.enter_context(tc.tile_pool(name="stage", bufs=4))
-        wpool = ctx.enter_context(tc.tile_pool(name="wpool", bufs=4))
-        psum = ctx.enter_context(tc.psum_pool(name="psum", bufs=8))
+        wpool = ctx.enter_context(tc.tile_pool(name="wpool", bufs=6))
+        psum = ctx.enter_context(tc.psum_pool(name="psum", bufs=1))
         ctx.enter_context(tc.manual_schedule())
 
         vec = keep.tile([P, BANK], BF16)
@@ -94,6 +97,27 @@ def tile_hyperlstmcell_pa_k_kernel(
         hc_sb = keep.tile([P, M_TILES, UNITS], BF16)
         nc.scalar.dma_start(out=hc_sb[:], in_=hyper_c.rearrange("(p m) k -> p m k", m=M_TILES))
 
+        def load_u(c):
+            source = x if c < U_CHUNKS // 2 else h
+            k0 = (c % (U_CHUNKS // 2)) * U_CHUNK * K_PASS
+            u_sb = stage.tile([P, M_TILES, U_CHUNK * K_PASS], BF16)
+            nc.sync.dma_start(
+                out=u_sb[:],
+                in_=source.rearrange("(p m) k -> p m k", m=M_TILES)[:, :, k0 : k0 + U_CHUNK * K_PASS],
+            )
+            return u_sb
+
+        w_bytes = hc_Wih_words.rearrange("g p n t -> p g (n t)")
+
+        def load_w_ifg(g0):
+            w_ifg = wpool.tile([P, W_CHUNK, N_IFG], U32, align_bytes=64)
+            nc.sync.dma_start(
+                out=w_ifg[:].bitcast(I32), in_=w_bytes[:, g0 : g0 + W_CHUNK, 0 : 4 * N_IFG].bitcast(I32)
+            )
+            return w_ifg
+
+        u_tiles = [load_u(0), load_u(1)]
+
         scale_rows = hc_Wih_scales.rearrange("(k j) q n -> q k j n", k=OFFSETS)
         for q in range(16):
             first = 32 * (q // 4) + q % 4
@@ -105,7 +129,7 @@ def tile_hyperlstmcell_pa_k_kernel(
         def row_selector(row):
             return ident_bf[:, row : row + 1].to_broadcast([P, P])
 
-        hhT_ps = psum.tile([P, M_TILES, 2, P], BF16, tag="bank")
+        hhT_ps = psum.tile([P, M_TILES, 2, P], BF16, tag="bank", bufs=T_BANKS)
         for m in range(M_TILES):
             for kh in range(2):
                 nc.tensor.transpose(hhT_ps[:, m, kh, :], hh_sb[:, m, kh * P : (kh + 1) * P], ident_bf[:])
@@ -114,7 +138,7 @@ def tile_hyperlstmcell_pa_k_kernel(
 
         whhT = keep.tile([P, 2, N], BF16)
         for kh in range(2):
-            whhT_ps = psum.tile([P, N // P, P], BF16, tag="bank")
+            whhT_ps = psum.tile([P, N // P, P], BF16, tag="bank", bufs=T_BANKS)
             for a in range(N // P):
                 nc.tensor.transpose(whhT_ps[:, a, :], whh_sb[:, a, kh * P : (kh + 1) * P], ident_bf[:])
             nc.vector.tensor_copy(
@@ -132,8 +156,8 @@ def tile_hyperlstmcell_pa_k_kernel(
             (ROW_BETA + 1, beta[:, BANK:N]),
             (ROW_CELL, cell_vec[:]),
         ]
-        for row, dest in spread:
-            spread_ps = psum.tile([P, BANK], F32, tag="bank")
+        for i, (row, dest) in enumerate(spread):
+            spread_ps = psum.tile([P, BANK], F32, tag="acc%d" % (i % 4))
             nc.tensor.matmul(spread_ps[:], lhsT=row_selector(row), rhs=vec[:], start=True, stop=True)
             nc.scalar.copy(out=dest, in_=spread_ps[:])
         nc.vector.tensor_scalar_add(out=beta[:, UNITS : 2 * UNITS], in0=beta[:, UNITS : 2 * UNITS], scalar1=1.0)
@@ -142,7 +166,7 @@ def tile_hyperlstmcell_pa_k_kernel(
         for m in range(M_TILES):
             for nh in range(N // BANK):
                 cols = slice(nh * BANK, (nh + 1) * BANK)
-                pre_ps = psum.tile([P, BANK], F32, tag="bank")
+                pre_ps = psum.tile([P, BANK], F32, tag="acc%d" % (2 * m + nh))
                 for kh in range(2):
                     nc.tensor.matmul(
                         pre_ps[:], lhsT=hhT[:, m, kh, :], rhs=whhT[:, kh, cols], start=(kh == 0), stop=False
@@ -152,40 +176,36 @@ def tile_hyperlstmcell_pa_k_kernel(
 
         u_codes = keep.tile([P, GROUPS, BATCH], U32, align_bytes=64)
         u_planes = keep.tile([P, GROUPS, BATCH], U8, align_bytes=64)
-        grouped_tiles = []
 
-        def quantise(g):
-            nc.vector.quantize_mx(
-                out=u_codes[:, g, :].bitcast(FP8X4), scales=u_planes[:, g, :], in_=grouped_tiles[g][:]
+        def regroup(u_sb):
+            u_words = stage.tile([P, M_TILES * U_CHUNK, 2, P], F32, bufs=2)
+            nc.vector.tensor_copy(
+                out=u_words[:],
+                in_=u_sb[:].rearrange("p m k -> p (m k)").bitcast(F32).rearrange("p (a q w) -> p a w q", w=2, q=P),
             )
+            return u_words
 
-        for g in range(GROUPS):
-            if g % U_CHUNK == 0:
-                source = x if g < GROUPS // 2 else h
-                k0 = (g % (GROUPS // 2)) * K_PASS
-                u_sb = stage.tile([P, M_TILES, U_CHUNK * K_PASS], BF16)
-                nc.sync.dma_start(
-                    out=u_sb[:],
-                    in_=source.rearrange("(p m) k -> p m k", m=M_TILES)[:, :, k0 : k0 + U_CHUNK * K_PASS],
+        def quantise(g, grouped):
+            nc.vector.quantize_mx(out=u_codes[:, g, :].bitcast(FP8X4), scales=u_planes[:, g, :], in_=grouped[:])
+
+        def transpose_and_quantise(c, u_words):
+            waiting = None
+            for gl in range(U_CHUNK):
+                g = c * U_CHUNK + gl
+                uT_ps = psum.tile([P, M_TILES, 2, P], F32, tag="bank", bufs=T_BANKS)
+                for m in range(M_TILES):
+                    for w in range(2):
+                        nc.tensor.transpose(uT_ps[:, m, w, :], u_words[:, m * U_CHUNK + gl, w, :], ident_f32[:])
+                grouped = stage.tile([P, 4 * BATCH], BF16, align_bytes=64)
+                copy = nc.vector.tensor_copy if gl == U_CHUNK - 1 else nc.scalar.copy
+                copy(
+                    out=grouped[:].bitcast(F32).rearrange("p (m r w) -> p m r w", m=M_TILES, w=2),
+                    in_=uT_ps[:].rearrange("p m w r -> p m r w"),
                 )
-            first_word = (g % U_CHUNK) * (K_PASS // 2)
-            uT_ps = psum.tile([P, M_TILES, 2, P], F32, tag="bank")
-            for m in range(M_TILES):
-                words = u_sb[:, m, :].bitcast(F32)
-                for w in range(2):
-                    nc.tensor.transpose(
-                        uT_ps[:, m, w, :], words[:, first_word + w : first_word + K_PASS // 2 : 2], ident_f32[:]
-                    )
-            grouped = stage.tile([P, 4 * BATCH], BF16, align_bytes=64)
-            grouped_tiles.append(grouped)
-            copy = nc.vector.tensor_copy if g % 4 == 3 else nc.scalar.copy
-            copy(
-                out=grouped[:].bitcast(F32).rearrange("p (m r w) -> p m r w", m=M_TILES, w=2),
-                in_=uT_ps[:].rearrange("p m w r -> p m r w"),
-            )
-            if g > 0:
-                quantise(g - 1)
-        quantise(GROUPS - 1)
+                if waiting is not None:
+                    quantise(*waiting)
+                waiting = (g, grouped)
+            quantise(*waiting)
 
         def mx_pass(acc, g, m, w_words, n_cols):
             kq, j = divmod(g, OFFSET_GROUPS)
@@ -200,26 +220,36 @@ def tile_hyperlstmcell_pa_k_kernel(
                 stop=(g == GROUPS - 1),
             )
 
-        w_bytes = hc_Wih_words.rearrange("g p n t -> p g (n t)")
-        acc_if = [psum.tile([P, 2 * UNITS], F32, tag="bank", name="acc_if%d" % m) for m in range(M_TILES)]
-        acc_g = [psum.tile([P, UNITS], F32, tag="bank", name="acc_g%d" % m) for m in range(M_TILES)]
-        acc_o = [psum.tile([P, UNITS], F32, tag="bank", name="acc_o%d" % m) for m in range(M_TILES)]
+        acc_if = [psum.tile([P, 2 * UNITS], F32, tag="acc%d" % m, name="acc_if%d" % m) for m in range(M_TILES)]
+        acc_g = [psum.tile([P, UNITS], F32, tag="acc%d" % (2 + m), name="acc_g%d" % m) for m in range(M_TILES)]
 
-        for g0 in range(0, GROUPS, W_CHUNK):
-            w_ifg = wpool.tile([P, W_CHUNK, N_IFG], U32, align_bytes=64)
-            nc.sync.dma_start(
-                out=w_ifg[:].bitcast(I32), in_=w_bytes[:, g0 : g0 + W_CHUNK, 0 : 4 * N_IFG].bitcast(I32)
-            )
+        def multiply_ifg(g0, w_ifg):
             for m in range(M_TILES):
                 for gl in range(W_CHUNK):
                     mx_pass(acc_if[m][:], g0 + gl, m, w_ifg[:, gl, 0 : 2 * UNITS], slice(0, 2 * UNITS))
                     mx_pass(acc_g[m][:], g0 + gl, m, w_ifg[:, gl, 2 * UNITS : N_IFG], slice(2 * UNITS, N_IFG))
 
+        for c in range(2):
+            transpose_and_quantise(c, regroup(u_tiles[c]))
+        for c in range(U_CHUNKS):
+            starts = range(c * U_CHUNK, (c + 1) * U_CHUNK, W_CHUNK)
+            w_tiles = [load_w_ifg(g0) for g0 in starts]
+            if c + 2 < U_CHUNKS:
+                next_u = load_u(c + 2)
+            for g0, w_ifg in zip(starts, w_tiles):
+                multiply_ifg(g0, w_ifg)
+            if c + 2 < U_CHUNKS:
+                transpose_and_quantise(c + 2, regroup(next_u))
+
+        acc_o = [
+            psum.tile([P, UNITS], F32, tag="bank", bufs=T_BANKS, name="acc_o%d" % m) for m in range(M_TILES)
+        ]
+
         w_o_tiles = []
-        for g0 in range(0, GROUPS, W_CHUNK):
-            w_o = wpool.tile([P, W_CHUNK, UNITS], U32, align_bytes=64, bufs=GROUPS // W_CHUNK)
+        for g0 in range(0, GROUPS, O_CHUNK):
+            w_o = wpool.tile([P, O_CHUNK, UNITS], U32, align_bytes=64, bufs=GROUPS // O_CHUNK)
             nc.sync.dma_start(
-                out=w_o[:].bitcast(I32), in_=w_bytes[:, g0 : g0 + W_CHUNK, 4 * N_IFG : 4 * N].bitcast(I32)
+                out=w_o[:].bitcast(I32), in_=w_bytes[:, g0 : g0 + O_CHUNK, 4 * N_IFG : 4 * N].bitcast(I32)
             )
             w_o_tiles.append(w_o)
 
@@ -318,10 +348,10 @@ def tile_hyperlstmcell_pa_k_kernel(
         for m in range(M_TILES):
             nc.scalar.activation(out=hidden[:, m, :], in_=cell[:, m, :], func=ACT.Tanh)
 
-        for c in range(GROUPS // W_CHUNK):
+        for c in range(GROUPS // O_CHUNK):
             for m in range(M_TILES):
-                for gl in range(W_CHUNK):
-                    mx_pass(acc_o[m][:], c * W_CHUNK + gl, m, w_o_tiles[c][:, gl, :], gate_cols(3))
+                for gl in range(O_CHUNK):
+                    mx_pass(acc_o[m][:], c * O_CHUNK + gl, m, w_o_tiles[c][:, gl, :], gate_cols(3))
         layer_norm("o", [[gate_row(m, 3, acc_o[m][:])] for m in range(M_TILES)], squares)
         for m in range(M_TILES):
             nc.scalar.activation(out=gates[:, m, gate_cols(3)], in_=gates[:, m, gate_cols(3)], func=ACT.Sigmoid)

@@ -68,21 +68,17 @@ def tile_hyperlstmcell_pa_k_kernel(
         psum = ctx.enter_context(tc.psum_pool(name="psum", bufs=1))
         ctx.enter_context(tc.manual_schedule())
 
-        vec = keep.tile([P, BANK], BF16)
-        nc.vector.memset(vec[:], 0.0)
-        w_planes = keep.tile([P, OFFSET_GROUPS, N], U8, align_bytes=64)
-        nc.vector.memset(w_planes[:].bitcast(I32), 0)
-        half = keep.tile([P, 8], F32)
-        nc.vector.memset(half[:], 0.5)
-        ident_bf = keep.tile([P, P], BF16)
-        make_identity(nc, ident_bf[:])
         ident_f32 = keep.tile([P, P], F32)
         make_identity(nc, ident_f32[:])
+        ident_bf = keep.tile([P, P], BF16)
+        make_identity(nc, ident_bf[:])
+        vec = keep.tile([P, BANK], BF16)
+        nc.vector.memset(vec[:], 0.0)
+        half = keep.tile([P, 8], F32)
+        nc.vector.memset(half[:], 0.5)
+        w_planes = keep.tile([P, OFFSET_GROUPS, N], U8, align_bytes=64)
+        nc.gpsimd.memset(w_planes[:].bitcast(I32), 0)
 
-        hh_sb = keep.tile([P, M_TILES, UNITS], BF16)
-        nc.sync.dma_start(out=hh_sb[:], in_=hyper_h.rearrange("(p m) k -> p m k", m=M_TILES))
-        whh_sb = keep.tile([P, N // P, UNITS], BF16)
-        nc.sync.dma_start(out=whh_sb[:], in_=hc_Whh.rearrange("(p a) k -> p a k", a=N // P))
         nc.scalar.dma_start(out=vec[ROW_BIAS : ROW_BIAS + 2, :], in_=hc_bih.rearrange("(a n) -> a n", a=2))
         nc.scalar.dma_start(
             out=vec[ROW_GAMMA : ROW_GAMMA + 2, :], in_=hc_ln_gamma.rearrange("(a b) n -> a (b n)", a=2)
@@ -97,14 +93,16 @@ def tile_hyperlstmcell_pa_k_kernel(
         hc_sb = keep.tile([P, M_TILES, UNITS], BF16)
         nc.scalar.dma_start(out=hc_sb[:], in_=hyper_c.rearrange("(p m) k -> p m k", m=M_TILES))
 
-        def load_u(c):
+        def load_u(c, parts):
             source = x if c < U_CHUNKS // 2 else h
             k0 = (c % (U_CHUNKS // 2)) * U_CHUNK * K_PASS
+            width = U_CHUNK * K_PASS // parts
             u_sb = stage.tile([P, M_TILES, U_CHUNK * K_PASS], BF16)
-            nc.sync.dma_start(
-                out=u_sb[:],
-                in_=source.rearrange("(p m) k -> p m k", m=M_TILES)[:, :, k0 : k0 + U_CHUNK * K_PASS],
-            )
+            for i in range(parts):
+                nc.sync.dma_start(
+                    out=u_sb[:, :, i * width : (i + 1) * width],
+                    in_=source.rearrange("(p m) k -> p m k", m=M_TILES)[:, :, k0 + i * width : k0 + (i + 1) * width],
+                )
             return u_sb
 
         w_bytes = hc_Wih_words.rearrange("g p n t -> p g (n t)")
@@ -116,7 +114,12 @@ def tile_hyperlstmcell_pa_k_kernel(
             )
             return w_ifg
 
-        u_tiles = [load_u(0), load_u(1)]
+        u_tiles = [load_u(0, 2)]
+        hh_sb = keep.tile([P, M_TILES, UNITS], BF16)
+        nc.sync.dma_start(out=hh_sb[:], in_=hyper_h.rearrange("(p m) k -> p m k", m=M_TILES))
+        whh_sb = keep.tile([P, N // P, UNITS], BF16)
+        nc.sync.dma_start(out=whh_sb[:], in_=hc_Whh.rearrange("(p a) k -> p a k", a=N // P))
+        u_tiles.append(load_u(1, 1))
 
         scale_rows = hc_Wih_scales.rearrange("(k j) q n -> q k j n", k=OFFSETS)
         for q in range(16):
@@ -125,6 +128,46 @@ def tile_hyperlstmcell_pa_k_kernel(
                 out=w_planes[first : first + 4 * OFFSETS : 4, :, :].bitcast(I32),
                 in_=scale_rows[q].bitcast(I32),
             )
+
+        u_codes = keep.tile([P, GROUPS, BATCH], U32, align_bytes=64)
+        u_planes = keep.tile([P, GROUPS, BATCH], U8, align_bytes=64)
+
+        def regroup(u_sb, parts):
+            u_words = stage.tile([P, M_TILES, U_CHUNK, 2, P], F32, bufs=2)
+            n = U_CHUNK // parts
+            for i in range(parts):
+                for m in range(M_TILES):
+                    nc.vector.tensor_copy(
+                        out=u_words[:, m, i * n : (i + 1) * n, :, :],
+                        in_=u_sb[:, m, i * n * K_PASS : (i + 1) * n * K_PASS]
+                        .bitcast(F32)
+                        .rearrange("p (a q w) -> p a w q", w=2, q=P),
+                    )
+            return u_words
+
+        def quantise(g, grouped):
+            nc.vector.quantize_mx(out=u_codes[:, g, :].bitcast(FP8X4), scales=u_planes[:, g, :], in_=grouped[:])
+
+        def transpose_and_quantise(c, u_words):
+            waiting = None
+            for gl in range(U_CHUNK):
+                g = c * U_CHUNK + gl
+                uT_ps = psum.tile([P, M_TILES, 2, P], F32, tag="bank", bufs=T_BANKS)
+                for m in range(M_TILES):
+                    for w in range(2):
+                        nc.tensor.transpose(uT_ps[:, m, w, :], u_words[:, m, gl, w, :], ident_f32[:])
+                grouped = stage.tile([P, 4 * BATCH], BF16, align_bytes=64)
+                copy = nc.vector.tensor_copy if gl == U_CHUNK - 1 else nc.scalar.copy
+                copy(
+                    out=grouped[:].bitcast(F32).rearrange("p (m r w) -> p m r w", m=M_TILES, w=2),
+                    in_=uT_ps[:].rearrange("p m w r -> p m r w"),
+                )
+                if waiting is not None:
+                    quantise(*waiting)
+                waiting = (g, grouped)
+            quantise(*waiting)
+
+        transpose_and_quantise(0, regroup(u_tiles[0], 2))
 
         def row_selector(row):
             return ident_bf[:, row : row + 1].to_broadcast([P, P])
@@ -174,39 +217,6 @@ def tile_hyperlstmcell_pa_k_kernel(
                 nc.tensor.matmul(pre_ps[:], lhsT=row_selector(ROW_BIAS + nh), rhs=vec[:], start=False, stop=True)
                 nc.scalar.copy(out=v[:, m, cols], in_=pre_ps[:])
 
-        u_codes = keep.tile([P, GROUPS, BATCH], U32, align_bytes=64)
-        u_planes = keep.tile([P, GROUPS, BATCH], U8, align_bytes=64)
-
-        def regroup(u_sb):
-            u_words = stage.tile([P, M_TILES * U_CHUNK, 2, P], F32, bufs=2)
-            nc.vector.tensor_copy(
-                out=u_words[:],
-                in_=u_sb[:].rearrange("p m k -> p (m k)").bitcast(F32).rearrange("p (a q w) -> p a w q", w=2, q=P),
-            )
-            return u_words
-
-        def quantise(g, grouped):
-            nc.vector.quantize_mx(out=u_codes[:, g, :].bitcast(FP8X4), scales=u_planes[:, g, :], in_=grouped[:])
-
-        def transpose_and_quantise(c, u_words):
-            waiting = None
-            for gl in range(U_CHUNK):
-                g = c * U_CHUNK + gl
-                uT_ps = psum.tile([P, M_TILES, 2, P], F32, tag="bank", bufs=T_BANKS)
-                for m in range(M_TILES):
-                    for w in range(2):
-                        nc.tensor.transpose(uT_ps[:, m, w, :], u_words[:, m * U_CHUNK + gl, w, :], ident_f32[:])
-                grouped = stage.tile([P, 4 * BATCH], BF16, align_bytes=64)
-                copy = nc.vector.tensor_copy if gl == U_CHUNK - 1 else nc.scalar.copy
-                copy(
-                    out=grouped[:].bitcast(F32).rearrange("p (m r w) -> p m r w", m=M_TILES, w=2),
-                    in_=uT_ps[:].rearrange("p m w r -> p m r w"),
-                )
-                if waiting is not None:
-                    quantise(*waiting)
-                waiting = (g, grouped)
-            quantise(*waiting)
-
         def mx_pass(acc, g, m, w_words, n_cols):
             kq, j = divmod(g, OFFSET_GROUPS)
             rows = slice(m * P, (m + 1) * P)
@@ -229,17 +239,16 @@ def tile_hyperlstmcell_pa_k_kernel(
                     mx_pass(acc_if[m][:], g0 + gl, m, w_ifg[:, gl, 0 : 2 * UNITS], slice(0, 2 * UNITS))
                     mx_pass(acc_g[m][:], g0 + gl, m, w_ifg[:, gl, 2 * UNITS : N_IFG], slice(2 * UNITS, N_IFG))
 
-        for c in range(2):
-            transpose_and_quantise(c, regroup(u_tiles[c]))
+        transpose_and_quantise(1, regroup(u_tiles[1], 1))
         for c in range(U_CHUNKS):
             starts = range(c * U_CHUNK, (c + 1) * U_CHUNK, W_CHUNK)
             w_tiles = [load_w_ifg(g0) for g0 in starts]
             if c + 2 < U_CHUNKS:
-                next_u = load_u(c + 2)
+                next_u = load_u(c + 2, 1)
             for g0, w_ifg in zip(starts, w_tiles):
                 multiply_ifg(g0, w_ifg)
             if c + 2 < U_CHUNKS:
-                transpose_and_quantise(c + 2, regroup(next_u))
+                transpose_and_quantise(c + 2, regroup(next_u, 1))
 
         acc_o = [
             psum.tile([P, UNITS], F32, tag="bank", bufs=T_BANKS, name="acc_o%d" % m) for m in range(M_TILES)

@@ -262,7 +262,7 @@ def tile_hyperlstmcell_pa_k_kernel(
             )
             w_o_tiles.append(w_o)
 
-        def layer_norm(label, rows_by_tile, squares):
+        def norm_steps(label, rows_by_tile):
             n = len(rows_by_tile[0])
             shape = [P, M_TILES, n]
             total = keep.tile(shape, F32, name="total_" + label)
@@ -270,37 +270,48 @@ def tile_hyperlstmcell_pa_k_kernel(
             sq_sum = keep.tile(shape, F32, name="sq_sum_" + label)
             root = keep.tile(shape, F32, name="root_" + label)
             rstd = keep.tile(shape, F32, name="rstd_" + label)
-            for m, rows in enumerate(rows_by_tile):
-                for i, row in enumerate(rows):
+
+            def add_up(m):
+                for i, row in enumerate(rows_by_tile[m]):
                     nc.vector.scalar_tensor_tensor(
                         out=row["s"], in0=row["first"], scalar=0.0, in1=row["second"],
                         op0=ALU.add, op1=ALU.add, accum_out=total[:, m, i : i + 1],
                     )
                 nc.vector.tensor_scalar_mul(out=neg_mean[:, m, :], in0=total[:, m, :], scalar1=-1.0 / UNITS)
-            for m, rows in enumerate(rows_by_tile):
-                for i, row in enumerate(rows):
+
+            def deviation(m):
+                for i, row in enumerate(rows_by_tile[m]):
                     nc.scalar.activation(
                         out=squares[:, m, i, :], in_=row["s"], func=ACT.Square,
                         bias=neg_mean[:, m, i : i + 1], accum_out=sq_sum[:, m, i : i + 1],
                     )
                 nc.gpsimd.tensor_tensor(out=root[:, m, :], in0=sq_sum[:, m, :], in1=half[:, 0:n], op=ALU.pow)
-            for m, rows in enumerate(rows_by_tile):
-                for i, row in enumerate(rows):
+
+            def centre(m):
+                for i, row in enumerate(rows_by_tile[m]):
                     nc.vector.scalar_tensor_tensor(
                         out=row["out"], in0=row["s"], scalar=neg_mean[:, m, i : i + 1], in1=row["gamma"],
                         op0=ALU.add, op1=ALU.mult,
                     )
-            for m, rows in enumerate(rows_by_tile):
+
+            def finish(m):
                 nc.vector.tensor_scalar(
                     out=rstd[:, m, :], in0=root[:, m, :], scalar1=1.0 / math.sqrt(UNITS - 1), scalar2=EPS,
                     op0=ALU.mult, op1=ALU.add,
                 )
                 nc.vector.reciprocal(out=rstd[:, m, :], in_=rstd[:, m, :])
-                for i, row in enumerate(rows):
+                for i, row in enumerate(rows_by_tile[m]):
                     nc.vector.scalar_tensor_tensor(
                         out=row["out"], in0=row["out"], scalar=rstd[:, m, i : i + 1], in1=row["beta"],
                         op0=ALU.mult, op1=ALU.add,
                     )
+
+            return add_up, deviation, centre, finish
+
+        def for_tiles(*steps):
+            for step in steps:
+                for m in range(M_TILES):
+                    step(m)
 
         def gate_cols(gate):
             return slice(gate * UNITS, (gate + 1) * UNITS)
@@ -318,7 +329,7 @@ def tile_hyperlstmcell_pa_k_kernel(
         cell = keep.tile([P, M_TILES, UNITS], F32)
         hidden = keep.tile([P, M_TILES, UNITS], F32)
 
-        layer_norm(
+        ifg_add_up, ifg_deviation, ifg_centre, ifg_finish = norm_steps(
             "ifg",
             [
                 [
@@ -328,19 +339,8 @@ def tile_hyperlstmcell_pa_k_kernel(
                 ]
                 for m in range(M_TILES)
             ],
-            squares,
         )
-        for m in range(M_TILES):
-            nc.scalar.activation(out=gates[:, m, 0 : 2 * UNITS], in_=gates[:, m, 0 : 2 * UNITS], func=ACT.Sigmoid)
-            nc.scalar.activation(out=gates[:, m, gate_cols(2)], in_=gates[:, m, gate_cols(2)], func=ACT.Tanh)
-        for m in range(M_TILES):
-            nc.vector.tensor_tensor(
-                out=forget_part[:, m, :], in0=gates[:, m, gate_cols(1)], in1=hc_sb[:, m, :], op=ALU.mult
-            )
-            nc.vector.tensor_tensor(
-                out=in_part[:, m, :], in0=gates[:, m, gate_cols(0)], in1=gates[:, m, gate_cols(2)], op=ALU.mult
-            )
-        layer_norm(
+        cell_add_up, cell_deviation, cell_centre, cell_finish = norm_steps(
             "cell",
             [
                 [
@@ -351,20 +351,45 @@ def tile_hyperlstmcell_pa_k_kernel(
                 ]
                 for m in range(M_TILES)
             ],
-            squares,
         )
-        nc.sync.dma_start(out=out_1.rearrange("(p m) c -> p m c", m=M_TILES), in_=cell[:])
-        for m in range(M_TILES):
+        o_add_up, o_deviation, o_centre, o_finish = norm_steps(
+            "o", [[gate_row(m, 3, acc_o[m][:])] for m in range(M_TILES)]
+        )
+
+        def squash_ifg(m):
+            nc.scalar.activation(out=gates[:, m, 0 : 2 * UNITS], in_=gates[:, m, 0 : 2 * UNITS], func=ACT.Sigmoid)
+            nc.scalar.activation(out=gates[:, m, gate_cols(2)], in_=gates[:, m, gate_cols(2)], func=ACT.Tanh)
+
+        def cell_parts(m):
+            nc.vector.tensor_tensor(
+                out=forget_part[:, m, :], in0=gates[:, m, gate_cols(1)], in1=hc_sb[:, m, :], op=ALU.mult
+            )
+            nc.vector.tensor_tensor(
+                out=in_part[:, m, :], in0=gates[:, m, gate_cols(0)], in1=gates[:, m, gate_cols(2)], op=ALU.mult
+            )
+            cell_add_up(m)
+
+        def squash_cell(m):
             nc.scalar.activation(out=hidden[:, m, :], in_=cell[:, m, :], func=ACT.Tanh)
+
+        def squash_o(m):
+            nc.scalar.activation(out=gates[:, m, gate_cols(3)], in_=gates[:, m, gate_cols(3)], func=ACT.Sigmoid)
+
+        def store_hidden(m):
+            nc.vector.tensor_tensor(
+                out=hidden[:, m, :], in0=hidden[:, m, :], in1=gates[:, m, gate_cols(3)], op=ALU.mult
+            )
+            nc.sync.dma_start(out=out_0.rearrange("(p m) c -> p m c", m=M_TILES)[:, m, :], in_=hidden[:, m, :])
+
+        for_tiles(ifg_add_up, ifg_deviation, ifg_centre, ifg_finish, squash_ifg)
+        for_tiles(cell_parts, cell_deviation, cell_centre)
 
         for c in range(GROUPS // O_CHUNK):
             for m in range(M_TILES):
                 for gl in range(O_CHUNK):
                     mx_pass(acc_o[m][:], c * O_CHUNK + gl, m, w_o_tiles[c][:, gl, :], gate_cols(3))
-        layer_norm("o", [[gate_row(m, 3, acc_o[m][:])] for m in range(M_TILES)], squares)
-        for m in range(M_TILES):
-            nc.scalar.activation(out=gates[:, m, gate_cols(3)], in_=gates[:, m, gate_cols(3)], func=ACT.Sigmoid)
-            nc.vector.tensor_tensor(
-                out=hidden[:, m, :], in0=hidden[:, m, :], in1=gates[:, m, gate_cols(3)], op=ALU.mult
-            )
-            nc.sync.dma_start(out=out_0.rearrange("(p m) c -> p m c", m=M_TILES)[:, m, :], in_=hidden[:, m, :])
+
+        for_tiles(o_add_up, o_deviation, o_centre)
+        for_tiles(cell_finish, squash_cell)
+        nc.sync.dma_start(out=out_1.rearrange("(p m) c -> p m c", m=M_TILES), in_=cell[:])
+        for_tiles(o_finish, squash_o, store_hidden)

@@ -23,14 +23,14 @@ GROUPS = K // K_PASS
 UNITS = 256
 GATES = 4
 N = GATES * UNITS
-N_IFG = 3 * UNITS
+N_IF = 2 * UNITS
 BANK = 512
 EPS = 1e-6
 
 U_CHUNK = 4
 U_CHUNKS = GROUPS // U_CHUNK
 W_CHUNK = 2
-O_CHUNK = 4
+GATE_CHUNK = 4
 T_BANKS = 4
 OFFSETS = 4
 OFFSET_GROUPS = GROUPS // OFFSETS
@@ -64,7 +64,7 @@ def tile_hyperlstmcell_pa_k_kernel(
     with ExitStack() as ctx:
         keep = ctx.enter_context(tc.tile_pool(name="keep", bufs=1))
         stage = ctx.enter_context(tc.tile_pool(name="stage", bufs=4))
-        wpool = ctx.enter_context(tc.tile_pool(name="wpool", bufs=6))
+        wpool = ctx.enter_context(tc.tile_pool(name="wpool", bufs=8))
         psum = ctx.enter_context(tc.psum_pool(name="psum", bufs=1))
         ctx.enter_context(tc.manual_schedule())
 
@@ -77,8 +77,9 @@ def tile_hyperlstmcell_pa_k_kernel(
         half = keep.tile([P, 8], F32)
         nc.vector.memset(half[:], 0.5)
         w_planes = keep.tile([P, OFFSET_GROUPS, N], U8, align_bytes=64)
-        nc.gpsimd.memset(w_planes[:].bitcast(I32), 0)
-
+        nc.vector.memset(w_planes[:].bitcast(I32), 0)
+        warm = keep.tile([P, 1], F32)
+        nc.scalar.activation(out=warm[:], in_=half[:, 0:1], func=ACT.Sigmoid)
         nc.scalar.dma_start(out=vec[ROW_BIAS : ROW_BIAS + 2, :], in_=hc_bih.rearrange("(a n) -> a n", a=2))
         nc.scalar.dma_start(
             out=vec[ROW_GAMMA : ROW_GAMMA + 2, :], in_=hc_ln_gamma.rearrange("(a b) n -> a (b n)", a=2)
@@ -107,18 +108,25 @@ def tile_hyperlstmcell_pa_k_kernel(
 
         w_bytes = hc_Wih_words.rearrange("g p n t -> p g (n t)")
 
-        def load_w_ifg(g0):
-            w_ifg = wpool.tile([P, W_CHUNK, N_IFG], U32, align_bytes=64)
+        def load_w_if(g0):
+            w_if = wpool.tile([P, W_CHUNK, N_IF], U32, align_bytes=64)
+            nc.sync.dma_start(out=w_if[:].bitcast(I32), in_=w_bytes[:, g0 : g0 + W_CHUNK, 0 : 4 * N_IF].bitcast(I32))
+            return w_if
+
+        def load_w_gate(gate, g0):
+            w_gate = wpool.tile([P, GATE_CHUNK, UNITS], U32, align_bytes=64, bufs=12)
             nc.sync.dma_start(
-                out=w_ifg[:].bitcast(I32), in_=w_bytes[:, g0 : g0 + W_CHUNK, 0 : 4 * N_IFG].bitcast(I32)
+                out=w_gate[:].bitcast(I32),
+                in_=w_bytes[:, g0 : g0 + GATE_CHUNK, 4 * gate * UNITS : 4 * (gate + 1) * UNITS].bitcast(I32),
             )
-            return w_ifg
+            return w_gate
 
         u_tiles = [load_u(0, 2)]
         hh_sb = keep.tile([P, M_TILES, UNITS], BF16)
         nc.sync.dma_start(out=hh_sb[:], in_=hyper_h.rearrange("(p m) k -> p m k", m=M_TILES))
         whh_sb = keep.tile([P, N // P, UNITS], BF16)
         nc.sync.dma_start(out=whh_sb[:], in_=hc_Whh.rearrange("(p a) k -> p a k", a=N // P))
+
         u_tiles.append(load_u(1, 1))
 
         scale_rows = hc_Wih_scales.rearrange("(k j) q n -> q k j n", k=OFFSETS)
@@ -168,9 +176,28 @@ def tile_hyperlstmcell_pa_k_kernel(
             quantise(*waiting)
 
         transpose_and_quantise(0, regroup(u_tiles[0], 2))
+        second_words = regroup(u_tiles[1], 1)
 
         def row_selector(row):
             return ident_bf[:, row : row + 1].to_broadcast([P, P])
+
+        bias = keep.tile([P, N], F32)
+        gamma = keep.tile([P, N], F32)
+        beta = keep.tile([P, N], F32)
+        cell_vec = keep.tile([P, 2 * UNITS], F32)
+
+        def spread_vectors(*rows):
+            for i, (row, dest) in enumerate(rows):
+                spread_ps = psum.tile([P, BANK], F32, tag="acc%d" % i)
+                nc.tensor.matmul(spread_ps[:], lhsT=row_selector(row), rhs=vec[:], start=True, stop=True)
+                nc.scalar.copy(out=dest, in_=spread_ps[:])
+
+        spread_vectors(
+            (ROW_BIAS, bias[:, 0:BANK]),
+            (ROW_BIAS + 1, bias[:, BANK:N]),
+            (ROW_GAMMA, gamma[:, 0:BANK]),
+            (ROW_GAMMA + 1, gamma[:, BANK:N]),
+        )
 
         hhT_ps = psum.tile([P, M_TILES, 2, P], BF16, tag="bank", bufs=T_BANKS)
         for m in range(M_TILES):
@@ -180,42 +207,28 @@ def tile_hyperlstmcell_pa_k_kernel(
         nc.vector.tensor_copy(out=hhT[:], in_=hhT_ps[:])
 
         whhT = keep.tile([P, 2, N], BF16)
-        for kh in range(2):
+        for kh, copy in enumerate((nc.scalar.copy, nc.vector.tensor_copy)):
             whhT_ps = psum.tile([P, N // P, P], BF16, tag="bank", bufs=T_BANKS)
             for a in range(N // P):
                 nc.tensor.transpose(whhT_ps[:, a, :], whh_sb[:, a, kh * P : (kh + 1) * P], ident_bf[:])
-            nc.vector.tensor_copy(
+            copy(
                 out=whhT[:, kh, :].rearrange("k (p a) -> k p a", a=N // P),
                 in_=whhT_ps[:].rearrange("k a p -> k p a"),
             )
 
-        gamma = keep.tile([P, N], F32)
-        beta = keep.tile([P, N], F32)
-        cell_vec = keep.tile([P, 2 * UNITS], F32)
-        spread = [
-            (ROW_GAMMA, gamma[:, 0:BANK]),
-            (ROW_GAMMA + 1, gamma[:, BANK:N]),
-            (ROW_BETA, beta[:, 0:BANK]),
-            (ROW_BETA + 1, beta[:, BANK:N]),
-            (ROW_CELL, cell_vec[:]),
-        ]
-        for i, (row, dest) in enumerate(spread):
-            spread_ps = psum.tile([P, BANK], F32, tag="acc%d" % (i % 4))
-            nc.tensor.matmul(spread_ps[:], lhsT=row_selector(row), rhs=vec[:], start=True, stop=True)
-            nc.scalar.copy(out=dest, in_=spread_ps[:])
-        nc.vector.tensor_scalar_add(out=beta[:, UNITS : 2 * UNITS], in0=beta[:, UNITS : 2 * UNITS], scalar1=1.0)
+        transpose_and_quantise(1, second_words)
+        spread_vectors((ROW_BETA, beta[:, 0:BANK]), (ROW_BETA + 1, beta[:, BANK:N]), (ROW_CELL, cell_vec[:]))
 
         v = keep.tile([P, M_TILES, N], F32)
         for m in range(M_TILES):
             for nh in range(N // BANK):
                 cols = slice(nh * BANK, (nh + 1) * BANK)
-                pre_ps = psum.tile([P, BANK], F32, tag="acc%d" % (2 * m + nh))
+                pre_ps = psum.tile([P, BANK], F32, tag="bank", bufs=T_BANKS)
                 for kh in range(2):
                     nc.tensor.matmul(
-                        pre_ps[:], lhsT=hhT[:, m, kh, :], rhs=whhT[:, kh, cols], start=(kh == 0), stop=False
+                        pre_ps[:], lhsT=hhT[:, m, kh, :], rhs=whhT[:, kh, cols], start=(kh == 0), stop=(kh == 1)
                     )
-                nc.tensor.matmul(pre_ps[:], lhsT=row_selector(ROW_BIAS + nh), rhs=vec[:], start=False, stop=True)
-                nc.scalar.copy(out=v[:, m, cols], in_=pre_ps[:])
+                nc.vector.tensor_tensor(out=v[:, m, cols], in0=pre_ps[:], in1=bias[:, cols], op=ALU.add)
 
         def mx_pass(acc, g, m, w_words, n_cols):
             kq, j = divmod(g, OFFSET_GROUPS)
@@ -233,34 +246,32 @@ def tile_hyperlstmcell_pa_k_kernel(
         acc_if = [psum.tile([P, 2 * UNITS], F32, tag="acc%d" % m, name="acc_if%d" % m) for m in range(M_TILES)]
         acc_g = [psum.tile([P, UNITS], F32, tag="acc%d" % (2 + m), name="acc_g%d" % m) for m in range(M_TILES)]
 
-        def multiply_ifg(g0, w_ifg):
+        def multiply(accs, g0, w_words, n_cols):
             for m in range(M_TILES):
-                for gl in range(W_CHUNK):
-                    mx_pass(acc_if[m][:], g0 + gl, m, w_ifg[:, gl, 0 : 2 * UNITS], slice(0, 2 * UNITS))
-                    mx_pass(acc_g[m][:], g0 + gl, m, w_ifg[:, gl, 2 * UNITS : N_IFG], slice(2 * UNITS, N_IFG))
+                for gl in range(w_words.shape[1]):
+                    mx_pass(accs[m][:], g0 + gl, m, w_words[:, gl, :], n_cols)
 
-        transpose_and_quantise(1, regroup(u_tiles[1], 1))
+        def gate_cols(gate):
+            return slice(gate * UNITS, (gate + 1) * UNITS)
+
         for c in range(U_CHUNKS):
             starts = range(c * U_CHUNK, (c + 1) * U_CHUNK, W_CHUNK)
-            w_tiles = [load_w_ifg(g0) for g0 in starts]
+            w_tiles = [load_w_if(g0) for g0 in starts]
             if c + 2 < U_CHUNKS:
                 next_u = load_u(c + 2, 1)
-            for g0, w_ifg in zip(starts, w_tiles):
-                multiply_ifg(g0, w_ifg)
+            for g0, w_if in zip(starts, w_tiles):
+                multiply(acc_if, g0, w_if, slice(0, N_IF))
             if c + 2 < U_CHUNKS:
                 transpose_and_quantise(c + 2, regroup(next_u, 1))
+
+        nc.vector.tensor_scalar_add(out=beta[:, UNITS : 2 * UNITS], in0=beta[:, UNITS : 2 * UNITS], scalar1=1.0)
 
         acc_o = [
             psum.tile([P, UNITS], F32, tag="bank", bufs=T_BANKS, name="acc_o%d" % m) for m in range(M_TILES)
         ]
 
-        w_o_tiles = []
-        for g0 in range(0, GROUPS, O_CHUNK):
-            w_o = wpool.tile([P, O_CHUNK, UNITS], U32, align_bytes=64, bufs=GROUPS // O_CHUNK)
-            nc.sync.dma_start(
-                out=w_o[:].bitcast(I32), in_=w_bytes[:, g0 : g0 + O_CHUNK, 4 * N_IFG : 4 * N].bitcast(I32)
-            )
-            w_o_tiles.append(w_o)
+        gate_starts = range(0, GROUPS, GATE_CHUNK)
+        w_g_tiles = [load_w_gate(2, g0) for g0 in gate_starts]
 
         def norm_steps(label, rows_by_tile):
             n = len(rows_by_tile[0])
@@ -313,9 +324,6 @@ def tile_hyperlstmcell_pa_k_kernel(
                 for m in range(M_TILES):
                     step(m)
 
-        def gate_cols(gate):
-            return slice(gate * UNITS, (gate + 1) * UNITS)
-
         def gate_row(m, gate, acc):
             return dict(
                 first=acc, second=v[:, m, gate_cols(gate)], s=v[:, m, gate_cols(gate)],
@@ -323,22 +331,17 @@ def tile_hyperlstmcell_pa_k_kernel(
             )
 
         gates = stage.tile([P, M_TILES, N], F32, tag="u_sb")
-        squares = stage.tile([P, M_TILES, 3, UNITS], F32, tag="u_sb")
+        squares = stage.tile([P, M_TILES, 2, UNITS], F32, tag="u_sb")
         forget_part = keep.tile([P, M_TILES, UNITS], F32)
         in_part = keep.tile([P, M_TILES, UNITS], F32)
         cell = keep.tile([P, M_TILES, UNITS], F32)
         hidden = keep.tile([P, M_TILES, UNITS], F32)
 
-        ifg_add_up, ifg_deviation, ifg_centre, ifg_finish = norm_steps(
-            "ifg",
-            [
-                [
-                    gate_row(m, 0, acc_if[m][:, 0:UNITS]),
-                    gate_row(m, 1, acc_if[m][:, UNITS : 2 * UNITS]),
-                    gate_row(m, 2, acc_g[m][:]),
-                ]
-                for m in range(M_TILES)
-            ],
+        if_add_up, if_deviation, if_centre, if_finish = norm_steps(
+            "if", [[gate_row(m, gate, acc_if[m][:, gate_cols(gate)]) for gate in range(2)] for m in range(M_TILES)]
+        )
+        g_add_up, g_deviation, g_centre, g_finish = norm_steps(
+            "g", [[gate_row(m, 2, acc_g[m][:])] for m in range(M_TILES)]
         )
         cell_add_up, cell_deviation, cell_centre, cell_finish = norm_steps(
             "cell",
@@ -356,24 +359,31 @@ def tile_hyperlstmcell_pa_k_kernel(
             "o", [[gate_row(m, 3, acc_o[m][:])] for m in range(M_TILES)]
         )
 
-        def squash_ifg(m):
-            nc.scalar.activation(out=gates[:, m, 0 : 2 * UNITS], in_=gates[:, m, 0 : 2 * UNITS], func=ACT.Sigmoid)
-            nc.scalar.activation(out=gates[:, m, gate_cols(2)], in_=gates[:, m, gate_cols(2)], func=ACT.Tanh)
+        def squash(m, cols, func):
+            nc.scalar.activation(out=gates[:, m, cols], in_=gates[:, m, cols], func=func)
 
-        def cell_parts(m):
-            nc.vector.tensor_tensor(
-                out=forget_part[:, m, :], in0=gates[:, m, gate_cols(1)], in1=hc_sb[:, m, :], op=ALU.mult
-            )
-            nc.vector.tensor_tensor(
-                out=in_part[:, m, :], in0=gates[:, m, gate_cols(0)], in1=gates[:, m, gate_cols(2)], op=ALU.mult
-            )
-            cell_add_up(m)
+        def squash_if(m):
+            squash(m, slice(0, N_IF), ACT.Sigmoid)
+
+        def squash_g(m):
+            squash(m, gate_cols(2), ACT.Tanh)
 
         def squash_cell(m):
             nc.scalar.activation(out=hidden[:, m, :], in_=cell[:, m, :], func=ACT.Tanh)
 
         def squash_o(m):
-            nc.scalar.activation(out=gates[:, m, gate_cols(3)], in_=gates[:, m, gate_cols(3)], func=ACT.Sigmoid)
+            squash(m, gate_cols(3), ACT.Sigmoid)
+
+        def forget(m):
+            nc.vector.tensor_tensor(
+                out=forget_part[:, m, :], in0=gates[:, m, gate_cols(1)], in1=hc_sb[:, m, :], op=ALU.mult
+            )
+
+        def take_in(m):
+            nc.vector.tensor_tensor(
+                out=in_part[:, m, :], in0=gates[:, m, gate_cols(0)], in1=gates[:, m, gate_cols(2)], op=ALU.mult
+            )
+            cell_add_up(m)
 
         def store_hidden(m):
             nc.vector.tensor_tensor(
@@ -381,15 +391,17 @@ def tile_hyperlstmcell_pa_k_kernel(
             )
             nc.sync.dma_start(out=out_0.rearrange("(p m) c -> p m c", m=M_TILES)[:, m, :], in_=hidden[:, m, :])
 
-        for_tiles(ifg_add_up, ifg_deviation, ifg_centre, ifg_finish, squash_ifg)
-        for_tiles(cell_parts, cell_deviation, cell_centre)
+        for_tiles(if_add_up, if_deviation, if_centre, if_finish, squash_if, forget)
 
-        for c in range(GROUPS // O_CHUNK):
-            for m in range(M_TILES):
-                for gl in range(O_CHUNK):
-                    mx_pass(acc_o[m][:], c * O_CHUNK + gl, m, w_o_tiles[c][:, gl, :], gate_cols(3))
+        w_o_tiles = []
+        for g0, w_g in zip(gate_starts, w_g_tiles):
+            multiply(acc_g, g0, w_g, gate_cols(2))
+            w_o_tiles.append(load_w_gate(3, g0))
 
-        for_tiles(o_add_up, o_deviation, o_centre)
-        for_tiles(cell_finish, squash_cell)
+        for_tiles(g_add_up, g_deviation, g_centre, g_finish, squash_g)
+        for_tiles(take_in, cell_deviation, cell_centre, cell_finish, squash_cell)
         nc.sync.dma_start(out=out_1.rearrange("(p m) c -> p m c", m=M_TILES), in_=cell[:])
-        for_tiles(o_finish, squash_o, store_hidden)
+
+        for g0, w_o in zip(gate_starts, w_o_tiles):
+            multiply(acc_o, g0, w_o, gate_cols(3))
+        for_tiles(o_add_up, o_deviation, o_centre, o_finish, squash_o, store_hidden)

@@ -78,8 +78,7 @@ def tile_hyperlstmcell_pa_k_kernel(
         nc.vector.memset(half[:], 0.5)
         w_planes = keep.tile([P, OFFSET_GROUPS, N], U8, align_bytes=64)
         nc.vector.memset(w_planes[:].bitcast(I32), 0)
-        warm = keep.tile([P, 1], F32)
-        nc.scalar.activation(out=warm[:], in_=half[:, 0:1], func=ACT.Sigmoid)
+
         nc.scalar.dma_start(out=vec[ROW_BIAS : ROW_BIAS + 2, :], in_=hc_bih.rearrange("(a n) -> a n", a=2))
         nc.scalar.dma_start(
             out=vec[ROW_GAMMA : ROW_GAMMA + 2, :], in_=hc_ln_gamma.rearrange("(a b) n -> a (b n)", a=2)
@@ -93,6 +92,9 @@ def tile_hyperlstmcell_pa_k_kernel(
         )
         hc_sb = keep.tile([P, M_TILES, UNITS], BF16)
         nc.scalar.dma_start(out=hc_sb[:], in_=hyper_c.rearrange("(p m) k -> p m k", m=M_TILES))
+
+        warm = keep.tile([P, 1], F32)
+        nc.scalar.activation(out=warm[:], in_=half[:, 0:1], func=ACT.Sigmoid)
 
         def load_u(c, parts):
             source = x if c < U_CHUNKS // 2 else h
@@ -127,7 +129,7 @@ def tile_hyperlstmcell_pa_k_kernel(
         whh_sb = keep.tile([P, N // P, UNITS], BF16)
         nc.sync.dma_start(out=whh_sb[:], in_=hc_Whh.rearrange("(p a) k -> p a k", a=N // P))
 
-        u_tiles.append(load_u(1, 1))
+        u_tiles += [load_u(1, 1), load_u(2, 1)]
 
         scale_rows = hc_Wih_scales.rearrange("(k j) q n -> q k j n", k=OFFSETS)
         for q in range(16):
@@ -176,7 +178,7 @@ def tile_hyperlstmcell_pa_k_kernel(
             quantise(*waiting)
 
         transpose_and_quantise(0, regroup(u_tiles[0], 2))
-        second_words = regroup(u_tiles[1], 1)
+        words = {1: regroup(u_tiles[1], 1)}
 
         def row_selector(row):
             return ident_bf[:, row : row + 1].to_broadcast([P, P])
@@ -216,7 +218,8 @@ def tile_hyperlstmcell_pa_k_kernel(
                 in_=whhT_ps[:].rearrange("k a p -> k p a"),
             )
 
-        transpose_and_quantise(1, second_words)
+        words[2] = regroup(u_tiles[2], 1)
+        transpose_and_quantise(1, words[1])
         spread_vectors((ROW_BETA, beta[:, 0:BANK]), (ROW_BETA + 1, beta[:, BANK:N]), (ROW_CELL, cell_vec[:]))
 
         v = keep.tile([P, M_TILES, N], F32)
@@ -257,12 +260,15 @@ def tile_hyperlstmcell_pa_k_kernel(
         for c in range(U_CHUNKS):
             starts = range(c * U_CHUNK, (c + 1) * U_CHUNK, W_CHUNK)
             w_tiles = [load_w_if(g0) for g0 in starts]
-            if c + 2 < U_CHUNKS:
-                next_u = load_u(c + 2, 1)
+            if c + 3 < U_CHUNKS:
+                next_u = load_u(c + 3, 1)
             for g0, w_if in zip(starts, w_tiles):
                 multiply(acc_if, g0, w_if, slice(0, N_IF))
-            if c + 2 < U_CHUNKS:
-                transpose_and_quantise(c + 2, regroup(next_u, 1))
+            if c + 3 < U_CHUNKS:
+                words[c + 3] = regroup(next_u, 1)
+                transpose_and_quantise(c + 2, words[c + 2])
+            if c + 3 == U_CHUNKS - 1:
+                transpose_and_quantise(c + 3, words[c + 3])
 
         nc.vector.tensor_scalar_add(out=beta[:, UNITS : 2 * UNITS], in0=beta[:, UNITS : 2 * UNITS], scalar1=1.0)
 

@@ -31,6 +31,7 @@ U_CHUNK = 4
 U_CHUNKS = GROUPS // U_CHUNK
 W_CHUNK = 2
 GATE_CHUNK = 4
+T_RUN = 2
 T_BANKS = 4
 OFFSETS = 4
 OFFSET_GROUPS = GROUPS // OFFSETS
@@ -158,10 +159,10 @@ def tile_hyperlstmcell_pa_k_kernel(
         def quantise(g, grouped):
             nc.vector.quantize_mx(out=u_codes[:, g, :].bitcast(FP8X4), scales=u_planes[:, g, :], in_=grouped[:])
 
-        def transpose_and_quantise(c, u_words):
+        def transpose_and_quantise(first, u_words):
             waiting = None
-            for gl in range(U_CHUNK):
-                g = c * U_CHUNK + gl
+            for g in range(first, first + T_RUN):
+                gl = g % U_CHUNK
                 uT_ps = psum.tile([P, M_TILES, 2, P], F32, tag="bank", bufs=T_BANKS)
                 for m in range(M_TILES):
                     for w in range(2):
@@ -177,8 +178,13 @@ def tile_hyperlstmcell_pa_k_kernel(
                 waiting = (g, grouped)
             quantise(*waiting)
 
-        transpose_and_quantise(0, regroup(u_tiles[0], 2))
-        words = {1: regroup(u_tiles[1], 1)}
+        def transpose_chunk(c):
+            for first in range(c * U_CHUNK, (c + 1) * U_CHUNK, T_RUN):
+                transpose_and_quantise(first, words[c])
+
+        words = {0: regroup(u_tiles[0], 2)}
+        transpose_chunk(0)
+        words[1] = regroup(u_tiles[1], 1)
 
         def row_selector(row):
             return ident_bf[:, row : row + 1].to_broadcast([P, P])
@@ -219,7 +225,7 @@ def tile_hyperlstmcell_pa_k_kernel(
             )
 
         words[2] = regroup(u_tiles[2], 1)
-        transpose_and_quantise(1, words[1])
+        transpose_chunk(1)
         spread_vectors((ROW_BETA, beta[:, 0:BANK]), (ROW_BETA + 1, beta[:, BANK:N]), (ROW_CELL, cell_vec[:]))
 
         v = keep.tile([P, M_TILES, N], F32)
@@ -257,18 +263,19 @@ def tile_hyperlstmcell_pa_k_kernel(
         def gate_cols(gate):
             return slice(gate * UNITS, (gate + 1) * UNITS)
 
-        for c in range(U_CHUNKS):
-            starts = range(c * U_CHUNK, (c + 1) * U_CHUNK, W_CHUNK)
-            w_tiles = [load_w_if(g0) for g0 in starts]
-            if c + 3 < U_CHUNKS:
-                next_u = load_u(c + 3, 1)
-            for g0, w_if in zip(starts, w_tiles):
-                multiply(acc_if, g0, w_if, slice(0, N_IF))
-            if c + 3 < U_CHUNKS:
-                words[c + 3] = regroup(next_u, 1)
-                transpose_and_quantise(c + 2, words[c + 2])
-            if c + 3 == U_CHUNKS - 1:
-                transpose_and_quantise(c + 3, words[c + 3])
+        transpose_chunk(2)
+        next_run = 3 * U_CHUNK
+        for g0 in range(0, GROUPS, W_CHUNK):
+            w_if = load_w_if(g0)
+            c = g0 // U_CHUNK + 3
+            if g0 % U_CHUNK == 0 and c < U_CHUNKS:
+                next_u = load_u(c, 1)
+            multiply(acc_if, g0, w_if, slice(0, N_IF))
+            if g0 % U_CHUNK == 0 and c < U_CHUNKS:
+                words[c] = regroup(next_u, 1)
+            if W_CHUNK <= g0 and next_run < GROUPS:
+                transpose_and_quantise(next_run, words[next_run // U_CHUNK])
+                next_run += T_RUN
 
         nc.vector.tensor_scalar_add(out=beta[:, UNITS : 2 * UNITS], in0=beta[:, UNITS : 2 * UNITS], scalar1=1.0)
 

@@ -26,6 +26,7 @@ N = GATES * UNITS
 N_IF = 2 * UNITS
 BANK = 512
 EPS = 1e-6
+MEAN_SCALE = -1.0 / UNITS
 
 U_CHUNK = 4
 U_CHUNKS = GROUPS // U_CHUNK
@@ -80,22 +81,22 @@ def tile_hyperlstmcell_pa_k_kernel(
         w_planes = keep.tile([P, OFFSET_GROUPS, N], U8, align_bytes=64)
         nc.vector.memset(w_planes[:].bitcast(I32), 0)
 
-        nc.scalar.dma_start(out=vec[ROW_BIAS : ROW_BIAS + 2, :], in_=hc_bih.rearrange("(a n) -> a n", a=2))
-        nc.scalar.dma_start(
+        warm = keep.tile([P, 1], F32)
+        nc.scalar.activation(out=warm[:], in_=half[:, 0:1], func=ACT.Sigmoid)
+
+        nc.gpsimd.dma_start(out=vec[ROW_BIAS : ROW_BIAS + 2, :], in_=hc_bih.rearrange("(a n) -> a n", a=2))
+        nc.gpsimd.dma_start(
             out=vec[ROW_GAMMA : ROW_GAMMA + 2, :], in_=hc_ln_gamma.rearrange("(a b) n -> a (b n)", a=2)
         )
-        nc.scalar.dma_start(
+        nc.gpsimd.dma_start(
             out=vec[ROW_BETA : ROW_BETA + 2, :], in_=hc_ln_beta.rearrange("(a b) n -> a (b n)", a=2)
         )
-        nc.scalar.dma_start(out=vec[ROW_CELL : ROW_CELL + 1, 0:UNITS], in_=hc_lnc_gamma.rearrange("(o n) -> o n", o=1))
-        nc.scalar.dma_start(
+        nc.gpsimd.dma_start(out=vec[ROW_CELL : ROW_CELL + 1, 0:UNITS], in_=hc_lnc_gamma.rearrange("(o n) -> o n", o=1))
+        nc.gpsimd.dma_start(
             out=vec[ROW_CELL : ROW_CELL + 1, UNITS : 2 * UNITS], in_=hc_lnc_beta.rearrange("(o n) -> o n", o=1)
         )
         hc_sb = keep.tile([P, M_TILES, UNITS], BF16)
-        nc.scalar.dma_start(out=hc_sb[:], in_=hyper_c.rearrange("(p m) k -> p m k", m=M_TILES))
-
-        warm = keep.tile([P, 1], F32)
-        nc.scalar.activation(out=warm[:], in_=half[:, 0:1], func=ACT.Sigmoid)
+        nc.gpsimd.dma_start(out=hc_sb[:], in_=hyper_c.rearrange("(p m) k -> p m k", m=M_TILES))
 
         def load_u(c, parts):
             source = x if c < U_CHUNKS // 2 else h
@@ -124,13 +125,13 @@ def tile_hyperlstmcell_pa_k_kernel(
             )
             return w_gate
 
-        u_tiles = [load_u(0, 2)]
+        u_tiles = [load_u(0, 4), load_u(1, 1)]
         hh_sb = keep.tile([P, M_TILES, UNITS], BF16)
         nc.sync.dma_start(out=hh_sb[:], in_=hyper_h.rearrange("(p m) k -> p m k", m=M_TILES))
         whh_sb = keep.tile([P, N // P, UNITS], BF16)
         nc.sync.dma_start(out=whh_sb[:], in_=hc_Whh.rearrange("(p a) k -> p a k", a=N // P))
 
-        u_tiles += [load_u(1, 1), load_u(2, 1)]
+        u_tiles.append(load_u(2, 1))
 
         scale_rows = hc_Wih_scales.rearrange("(k j) q n -> q k j n", k=OFFSETS)
         for q in range(16):
@@ -182,9 +183,10 @@ def tile_hyperlstmcell_pa_k_kernel(
             for first in range(c * U_CHUNK, (c + 1) * U_CHUNK, T_RUN):
                 transpose_and_quantise(first, words[c])
 
-        words = {0: regroup(u_tiles[0], 2)}
+        words = {0: regroup(u_tiles[0], 4), 1: regroup(u_tiles[1], 1)}
         transpose_chunk(0)
-        words[1] = regroup(u_tiles[1], 1)
+        words[2] = regroup(u_tiles[2], 1)
+        transpose_chunk(1)
 
         def row_selector(row):
             return ident_bf[:, row : row + 1].to_broadcast([P, P])
@@ -195,49 +197,61 @@ def tile_hyperlstmcell_pa_k_kernel(
         cell_vec = keep.tile([P, 2 * UNITS], F32)
 
         def spread_vectors(*rows):
-            for i, (row, dest) in enumerate(rows):
+            for i, (row, *parts) in enumerate(rows):
                 spread_ps = psum.tile([P, BANK], F32, tag="acc%d" % i)
                 nc.tensor.matmul(spread_ps[:], lhsT=row_selector(row), rhs=vec[:], start=True, stop=True)
-                nc.scalar.copy(out=dest, in_=spread_ps[:])
+                start = 0
+                for dest, factor in parts:
+                    end = start + dest.shape[1]
+                    nc.scalar.mul(dest, spread_ps[:, start:end], factor)
+                    start = end
 
-        spread_vectors(
-            (ROW_BIAS, bias[:, 0:BANK]),
-            (ROW_BIAS + 1, bias[:, BANK:N]),
-            (ROW_GAMMA, gamma[:, 0:BANK]),
-            (ROW_GAMMA + 1, gamma[:, BANK:N]),
-        )
-
-        hhT_ps = psum.tile([P, M_TILES, 2, P], BF16, tag="bank", bufs=T_BANKS)
+        hhT_ps = psum.tile([P, M_TILES, P], F32, tag="acc0")
         for m in range(M_TILES):
-            for kh in range(2):
-                nc.tensor.transpose(hhT_ps[:, m, kh, :], hh_sb[:, m, kh * P : (kh + 1) * P], ident_bf[:])
-        hhT = keep.tile([P, M_TILES, 2, P], BF16)
-        nc.vector.tensor_copy(out=hhT[:], in_=hhT_ps[:])
+            nc.tensor.transpose(hhT_ps[:, m, :], hh_sb[:, m, :].bitcast(F32), ident_f32[:])
+        hhT = keep.tile([P, M_TILES * P], F32)
+        nc.vector.tensor_copy(out=hhT[:], in_=hhT_ps[:].rearrange("q m r -> q (m r)"))
+        hhT_k = hhT[:].bitcast(BF16).rearrange("q (b e) -> q e b", e=2)
 
-        whhT = keep.tile([P, 2, N], BF16)
-        for kh, copy in enumerate((nc.scalar.copy, nc.vector.tensor_copy)):
-            whhT_ps = psum.tile([P, N // P, P], BF16, tag="bank", bufs=T_BANKS)
-            for a in range(N // P):
-                nc.tensor.transpose(whhT_ps[:, a, :], whh_sb[:, a, kh * P : (kh + 1) * P], ident_bf[:])
+        whhT = keep.tile([P, N], F32)
+        n_blocks = N // P
+        for half_of_a, copy in enumerate((nc.scalar.copy, nc.vector.tensor_copy)):
+            blocks = slice(half_of_a * n_blocks // 2, (half_of_a + 1) * n_blocks // 2)
+            whhT_ps = psum.tile([P, n_blocks // 2, P], F32, tag="acc%d" % (1 + half_of_a))
+            for i, a in enumerate(range(blocks.start, blocks.stop)):
+                nc.tensor.transpose(whhT_ps[:, i, :], whh_sb[:, a, :].bitcast(F32), ident_f32[:])
             copy(
-                out=whhT[:, kh, :].rearrange("k (p a) -> k p a", a=N // P),
-                in_=whhT_ps[:].rearrange("k a p -> k p a"),
+                out=whhT[:].rearrange("q (p a) -> q p a", a=n_blocks)[:, :, blocks],
+                in_=whhT_ps[:].rearrange("q a p -> q p a"),
             )
+        whhT_k = whhT[:].bitcast(BF16).rearrange("q (n e) -> q e n", e=2)
 
-        words[2] = regroup(u_tiles[2], 1)
-        transpose_chunk(1)
-        spread_vectors((ROW_BETA, beta[:, 0:BANK]), (ROW_BETA + 1, beta[:, BANK:N]), (ROW_CELL, cell_vec[:]))
+        transpose_chunk(2)
+        spread_vectors(
+            (ROW_BIAS, (bias[:, 0:BANK], MEAN_SCALE)),
+            (ROW_BIAS + 1, (bias[:, BANK:N], MEAN_SCALE)),
+            (ROW_GAMMA, (gamma[:, 0:BANK], 1.0 / MEAN_SCALE)),
+            (ROW_GAMMA + 1, (gamma[:, BANK:N], 1.0 / MEAN_SCALE)),
+        )
+        spread_vectors(
+            (ROW_BETA, (beta[:, 0:BANK], 1.0)),
+            (ROW_BETA + 1, (beta[:, BANK:N], 1.0)),
+            (ROW_CELL, (cell_vec[:, 0:UNITS], 1.0 / MEAN_SCALE), (cell_vec[:, UNITS : 2 * UNITS], 1.0)),
+        )
 
         v = keep.tile([P, M_TILES, N], F32)
         for m in range(M_TILES):
             for nh in range(N // BANK):
                 cols = slice(nh * BANK, (nh + 1) * BANK)
                 pre_ps = psum.tile([P, BANK], F32, tag="bank", bufs=T_BANKS)
-                for kh in range(2):
+                for e in range(2):
                     nc.tensor.matmul(
-                        pre_ps[:], lhsT=hhT[:, m, kh, :], rhs=whhT[:, kh, cols], start=(kh == 0), stop=(kh == 1)
+                        pre_ps[:], lhsT=hhT_k[:, e, m * P : (m + 1) * P], rhs=whhT_k[:, e, cols],
+                        start=(e == 0), stop=(e == 1),
                     )
-                nc.vector.tensor_tensor(out=v[:, m, cols], in0=pre_ps[:], in1=bias[:, cols], op=ALU.add)
+                nc.vector.scalar_tensor_tensor(
+                    out=v[:, m, cols], in0=pre_ps[:], scalar=MEAN_SCALE, in1=bias[:, cols], op0=ALU.mult, op1=ALU.add
+                )
 
         def mx_pass(acc, g, m, w_words, n_cols):
             kq, j = divmod(g, OFFSET_GROUPS)
@@ -263,7 +277,6 @@ def tile_hyperlstmcell_pa_k_kernel(
         def gate_cols(gate):
             return slice(gate * UNITS, (gate + 1) * UNITS)
 
-        transpose_chunk(2)
         next_run = 3 * U_CHUNK
         for g0 in range(0, GROUPS, W_CHUNK):
             w_if = load_w_if(g0)
@@ -289,8 +302,8 @@ def tile_hyperlstmcell_pa_k_kernel(
         def norm_steps(label, rows_by_tile):
             n = len(rows_by_tile[0])
             shape = [P, M_TILES, n]
-            total = keep.tile(shape, F32, name="total_" + label)
             neg_mean = keep.tile(shape, F32, name="neg_mean_" + label)
+            shift = keep.tile(shape, F32, name="shift_" + label)
             sq_sum = keep.tile(shape, F32, name="sq_sum_" + label)
             root = keep.tile(shape, F32, name="root_" + label)
             rstd = keep.tile(shape, F32, name="rstd_" + label)
@@ -298,23 +311,23 @@ def tile_hyperlstmcell_pa_k_kernel(
             def add_up(m):
                 for i, row in enumerate(rows_by_tile[m]):
                     nc.vector.scalar_tensor_tensor(
-                        out=row["s"], in0=row["first"], scalar=0.0, in1=row["second"],
-                        op0=ALU.add, op1=ALU.add, accum_out=total[:, m, i : i + 1],
+                        out=row["s"], in0=row["first"], scalar=MEAN_SCALE, in1=row["second"],
+                        op0=ALU.mult, op1=ALU.add, accum_out=neg_mean[:, m, i : i + 1],
                     )
-                nc.vector.tensor_scalar_mul(out=neg_mean[:, m, :], in0=total[:, m, :], scalar1=-1.0 / UNITS)
 
             def deviation(m):
                 for i, row in enumerate(rows_by_tile[m]):
                     nc.scalar.activation(
-                        out=squares[:, m, i, :], in_=row["s"], func=ACT.Square,
+                        out=squares[:, m, i, :], in_=row["s"], func=ACT.Square, scale=1.0 / MEAN_SCALE,
                         bias=neg_mean[:, m, i : i + 1], accum_out=sq_sum[:, m, i : i + 1],
                     )
                 nc.gpsimd.tensor_tensor(out=root[:, m, :], in0=sq_sum[:, m, :], in1=half[:, 0:n], op=ALU.pow)
 
             def centre(m):
+                nc.vector.tensor_scalar_mul(out=shift[:, m, :], in0=neg_mean[:, m, :], scalar1=MEAN_SCALE)
                 for i, row in enumerate(rows_by_tile[m]):
                     nc.vector.scalar_tensor_tensor(
-                        out=row["out"], in0=row["s"], scalar=neg_mean[:, m, i : i + 1], in1=row["gamma"],
+                        out=row["out"], in0=row["s"], scalar=shift[:, m, i : i + 1], in1=row["gamma"],
                         op0=ALU.add, op1=ALU.mult,
                     )
 
@@ -393,8 +406,9 @@ def tile_hyperlstmcell_pa_k_kernel(
             )
 
         def take_in(m):
-            nc.vector.tensor_tensor(
-                out=in_part[:, m, :], in0=gates[:, m, gate_cols(0)], in1=gates[:, m, gate_cols(2)], op=ALU.mult
+            nc.vector.scalar_tensor_tensor(
+                out=in_part[:, m, :], in0=gates[:, m, gate_cols(0)], scalar=MEAN_SCALE, in1=gates[:, m, gate_cols(2)],
+                op0=ALU.mult, op1=ALU.mult,
             )
             cell_add_up(m)
 

import math
from contextlib import ExitStack

import concourse.mybir as mybir
from concourse.masks import make_identity

F32 = mybir.dt.float32
BF16 = mybir.dt.bfloat16
I32 = mybir.dt.int32
U32 = mybir.dt.uint32
U8 = mybir.dt.uint8
FP8X4 = mybir.dt.float8_e4m3fn_x4
ALU = mybir.AluOpType
ACT = mybir.ActivationFunctionType

P = 128
BATCH = 256
M_TILES = BATCH // P
IN = 8192
K = 2 * IN
K_PASS = 4 * P
GROUPS = K // K_PASS
UNITS = 256
GATES = 4
N = GATES * UNITS
N_IF = 2 * UNITS
BANK = 512
EPS = 1e-6
MEAN_SCALE = -1.0 / UNITS

U_CHUNK = 4
U_CHUNKS = GROUPS // U_CHUNK
W_CHUNK = 2
GATE_CHUNK = 4
T_RUN = 2
T_BANKS = 4
OFFSETS = 4
OFFSET_GROUPS = GROUPS // OFFSETS

ROW_BIAS = 0
ROW_GAMMA = 2
ROW_BETA = 4
ROW_CELL = 6

FLOPS = 2 * BATCH * K * N + 2 * BATCH * UNITS * N


def tile_hyperlstmcell_pa_k_kernel(
    tc,
    x,
    h,
    hyper_h,
    hyper_c,
    hc_Wih_words,
    hc_Wih_scales,
    hc_bih,
    hc_Whh,
    hc_ln_gamma,
    hc_ln_beta,
    hc_lnc_gamma,
    hc_lnc_beta,
    out_0,
    out_1,
):
    nc = tc.nc
    with ExitStack() as ctx:
        keep = ctx.enter_context(tc.tile_pool(name="keep", bufs=1))
        stage = ctx.enter_context(tc.tile_pool(name="stage", bufs=4))
        wpool = ctx.enter_context(tc.tile_pool(name="wpool", bufs=8))
        psum = ctx.enter_context(tc.psum_pool(name="psum", bufs=1))
        ctx.enter_context(tc.manual_schedule())

        ident_f32 = keep.tile([P, P], F32)
        make_identity(nc, ident_f32[:])
        ident_bf = keep.tile([P, P], BF16)
        make_identity(nc, ident_bf[:])
        vec = keep.tile([P, BANK], BF16)
        nc.vector.memset(vec[:], 0.0)
        half = keep.tile([P, 8], F32)
        nc.vector.memset(half[:], 0.5)
        w_planes = keep.tile([P, OFFSET_GROUPS, N], U8, align_bytes=64)
        nc.vector.memset(w_planes[:].bitcast(I32), 0)

        warm = keep.tile([P, 1], F32)
        nc.scalar.activation(out=warm[:], in_=half[:, 0:1], func=ACT.Sigmoid)

        nc.gpsimd.dma_start(out=vec[ROW_BIAS : ROW_BIAS + 2, :], in_=hc_bih.rearrange("(a n) -> a n", a=2))
        nc.gpsimd.dma_start(
            out=vec[ROW_GAMMA : ROW_GAMMA + 2, :], in_=hc_ln_gamma.rearrange("(a b) n -> a (b n)", a=2)
        )
        nc.gpsimd.dma_start(
            out=vec[ROW_BETA : ROW_BETA + 2, :], in_=hc_ln_beta.rearrange("(a b) n -> a (b n)", a=2)
        )
        nc.gpsimd.dma_start(out=vec[ROW_CELL : ROW_CELL + 1, 0:UNITS], in_=hc_lnc_gamma.rearrange("(o n) -> o n", o=1))
        nc.gpsimd.dma_start(
            out=vec[ROW_CELL : ROW_CELL + 1, UNITS : 2 * UNITS], in_=hc_lnc_beta.rearrange("(o n) -> o n", o=1)
        )
        hc_sb = keep.tile([P, M_TILES, UNITS], BF16)
        nc.gpsimd.dma_start(out=hc_sb[:], in_=hyper_c.rearrange("(p m) k -> p m k", m=M_TILES))

        def load_u(c, parts):
            source = x if c < U_CHUNKS // 2 else h
            k0 = (c % (U_CHUNKS // 2)) * U_CHUNK * K_PASS
            width = U_CHUNK * K_PASS // parts
            u_sb = stage.tile([P, M_TILES, U_CHUNK * K_PASS], BF16)
            for i in range(parts):
                nc.sync.dma_start(
                    out=u_sb[:, :, i * width : (i + 1) * width],
                    in_=source.rearrange("(p m) k -> p m k", m=M_TILES)[:, :, k0 + i * width : k0 + (i + 1) * width],
                )
            return u_sb

        w_bytes = hc_Wih_words.rearrange("g p n t -> p g (n t)")

        def load_w_if(g0):
            w_if = wpool.tile([P, W_CHUNK, N_IF], U32, align_bytes=64)
            nc.sync.dma_start(out=w_if[:].bitcast(I32), in_=w_bytes[:, g0 : g0 + W_CHUNK, 0 : 4 * N_IF].bitcast(I32))
            return w_if

        def load_w_gate(gate, g0):
            w_gate = wpool.tile([P, GATE_CHUNK, UNITS], U32, align_bytes=64, bufs=12)
            nc.sync.dma_start(
                out=w_gate[:].bitcast(I32),
                in_=w_bytes[:, g0 : g0 + GATE_CHUNK, 4 * gate * UNITS : 4 * (gate + 1) * UNITS].bitcast(I32),
            )
            return w_gate

        u_tiles = [load_u(0, 4), load_u(1, 1)]
        hh_sb = keep.tile([P, M_TILES, UNITS], BF16)
        nc.sync.dma_start(out=hh_sb[:], in_=hyper_h.rearrange("(p m) k -> p m k", m=M_TILES))
        whh_sb = keep.tile([P, N // P, UNITS], BF16)
        nc.sync.dma_start(out=whh_sb[:], in_=hc_Whh.rearrange("(p a) k -> p a k", a=N // P))

        u_tiles.append(load_u(2, 1))

        scale_rows = hc_Wih_scales.rearrange("(k j) q n -> q k j n", k=OFFSETS)
        for q in range(16):
            first = 32 * (q // 4) + q % 4
            nc.sync.dma_start(
                out=w_planes[first : first + 4 * OFFSETS : 4, :, :].bitcast(I32),
                in_=scale_rows[q].bitcast(I32),
            )

        u_codes = keep.tile([P, GROUPS, BATCH], U32, align_bytes=64)
        u_planes = keep.tile([P, GROUPS, BATCH], U8, align_bytes=64)

        def regroup(u_sb, parts):
            u_words = stage.tile([P, M_TILES, U_CHUNK, 2, P], F32, bufs=2)
            n = U_CHUNK // parts
            for i in range(parts):
                for m in range(M_TILES):
                    nc.vector.tensor_copy(
                        out=u_words[:, m, i * n : (i + 1) * n, :, :],
                        in_=u_sb[:, m, i * n * K_PASS : (i + 1) * n * K_PASS]
                        .bitcast(F32)
                        .rearrange("p (a q w) -> p a w q", w=2, q=P),
                    )
            return u_words

        def quantise(g, grouped):
            nc.vector.quantize_mx(out=u_codes[:, g, :].bitcast(FP8X4), scales=u_planes[:, g, :], in_=grouped[:])

        def transpose_and_quantise(first, u_words):
            waiting = None
            for g in range(first, first + T_RUN):
                gl = g % U_CHUNK
                uT_ps = psum.tile([P, M_TILES, 2, P], F32, tag="bank", bufs=T_BANKS)
                for m in range(M_TILES):
                    for w in range(2):
                        nc.tensor.transpose(uT_ps[:, m, w, :], u_words[:, m, gl, w, :], ident_f32[:])
                grouped = stage.tile([P, 4 * BATCH], BF16, align_bytes=64)
                copy = nc.vector.tensor_copy if gl == U_CHUNK - 1 else nc.scalar.copy
                copy(
                    out=grouped[:].bitcast(F32).rearrange("p (m r w) -> p m r w", m=M_TILES, w=2),
                    in_=uT_ps[:].rearrange("p m w r -> p m r w"),
                )
                if waiting is not None:
                    quantise(*waiting)
                waiting = (g, grouped)
            quantise(*waiting)

        def transpose_chunk(c):
            for first in range(c * U_CHUNK, (c + 1) * U_CHUNK, T_RUN):
                transpose_and_quantise(first, words[c])

        words = {0: regroup(u_tiles[0], 4), 1: regroup(u_tiles[1], 1)}
        transpose_chunk(0)
        words[2] = regroup(u_tiles[2], 1)
        transpose_chunk(1)

        def row_selector(row):
            return ident_bf[:, row : row + 1].to_broadcast([P, P])

        bias = keep.tile([P, N], F32)
        gamma = keep.tile([P, N], F32)
        beta = keep.tile([P, N], F32)
        cell_vec = keep.tile([P, 2 * UNITS], F32)

        def spread_vectors(*rows):
            for i, (row, *parts) in enumerate(rows):
                spread_ps = psum.tile([P, BANK], F32, tag="acc%d" % i)
                nc.tensor.matmul(spread_ps[:], lhsT=row_selector(row), rhs=vec[:], start=True, stop=True)
                start = 0
                for dest, factor in parts:
                    end = start + dest.shape[1]
                    nc.scalar.mul(dest, spread_ps[:, start:end], factor)
                    start = end

        hhT_ps = psum.tile([P, M_TILES, P], F32, tag="acc0")
        for m in range(M_TILES):
            nc.tensor.transpose(hhT_ps[:, m, :], hh_sb[:, m, :].bitcast(F32), ident_f32[:])
        hhT = keep.tile([P, M_TILES * P], F32)
        nc.vector.tensor_copy(out=hhT[:], in_=hhT_ps[:].rearrange("q m r -> q (m r)"))
        hhT_k = hhT[:].bitcast(BF16).rearrange("q (b e) -> q e b", e=2)

        whhT = keep.tile([P, N], F32)
        n_blocks = N // P
        for half_of_a, copy in enumerate((nc.scalar.copy, nc.vector.tensor_copy)):
            blocks = slice(half_of_a * n_blocks // 2, (half_of_a + 1) * n_blocks // 2)
            whhT_ps = psum.tile([P, n_blocks // 2, P], F32, tag="acc%d" % (1 + half_of_a))
            for i, a in enumerate(range(blocks.start, blocks.stop)):
                nc.tensor.transpose(whhT_ps[:, i, :], whh_sb[:, a, :].bitcast(F32), ident_f32[:])
            copy(
                out=whhT[:].rearrange("q (p a) -> q p a", a=n_blocks)[:, :, blocks],
                in_=whhT_ps[:].rearrange("q a p -> q p a"),
            )
        whhT_k = whhT[:].bitcast(BF16).rearrange("q (n e) -> q e n", e=2)

        transpose_chunk(2)
        spread_vectors(
            (ROW_BIAS, (bias[:, 0:BANK], MEAN_SCALE)),
            (ROW_BIAS + 1, (bias[:, BANK:N], MEAN_SCALE)),
            (ROW_GAMMA, (gamma[:, 0:BANK], 1.0 / MEAN_SCALE)),
            (ROW_GAMMA + 1, (gamma[:, BANK:N], 1.0 / MEAN_SCALE)),
        )
        spread_vectors(
            (ROW_BETA, (beta[:, 0:BANK], 1.0)),
            (ROW_BETA + 1, (beta[:, BANK:N], 1.0)),
            (ROW_CELL, (cell_vec[:, 0:UNITS], 1.0 / MEAN_SCALE), (cell_vec[:, UNITS : 2 * UNITS], 1.0)),
        )

        v = keep.tile([P, M_TILES, N], F32)
        for m in range(M_TILES):
            for nh in range(N // BANK):
                cols = slice(nh * BANK, (nh + 1) * BANK)
                pre_ps = psum.tile([P, BANK], F32, tag="bank", bufs=T_BANKS)
                for e in range(2):
                    nc.tensor.matmul(
                        pre_ps[:], lhsT=hhT_k[:, e, m * P : (m + 1) * P], rhs=whhT_k[:, e, cols],
                        start=(e == 0), stop=(e == 1),
                    )
                nc.vector.scalar_tensor_tensor(
                    out=v[:, m, cols], in0=pre_ps[:], scalar=MEAN_SCALE, in1=bias[:, cols], op0=ALU.mult, op1=ALU.add
                )

        def mx_pass(acc, g, m, w_words, n_cols):
            kq, j = divmod(g, OFFSET_GROUPS)
            rows = slice(m * P, (m + 1) * P)
            nc.tensor.matmul_mx(
                out=acc,
                lhsT=u_codes[:, g, rows].bitcast(FP8X4),
                lhsT_scale=u_planes[:, g, rows],
                rhs=w_words.bitcast(FP8X4),
                rhs_scale=w_planes[4 * kq : P, j, n_cols],
                start=(g == 0),
                stop=(g == GROUPS - 1),
            )

        acc_if = [psum.tile([P, 2 * UNITS], F32, tag="acc%d" % m, name="acc_if%d" % m) for m in range(M_TILES)]
        acc_g = [psum.tile([P, UNITS], F32, tag="acc%d" % (2 + m), name="acc_g%d" % m) for m in range(M_TILES)]

        def multiply(accs, g0, w_words, n_cols):
            for m in range(M_TILES):
                for gl in range(w_words.shape[1]):
                    mx_pass(accs[m][:], g0 + gl, m, w_words[:, gl, :], n_cols)

        def gate_cols(gate):
            return slice(gate * UNITS, (gate + 1) * UNITS)

        next_run = 3 * U_CHUNK
        for g0 in range(0, GROUPS, W_CHUNK):
            w_if = load_w_if(g0)
            c = g0 // U_CHUNK + 3
            if g0 % U_CHUNK == 0 and c < U_CHUNKS:
                next_u = load_u(c, 1)
            multiply(acc_if, g0, w_if, slice(0, N_IF))
            if g0 % U_CHUNK == 0 and c < U_CHUNKS:
                words[c] = regroup(next_u, 1)
            if W_CHUNK <= g0 and next_run < GROUPS:
                transpose_and_quantise(next_run, words[next_run // U_CHUNK])
                next_run += T_RUN

        nc.vector.tensor_scalar_add(out=beta[:, UNITS : 2 * UNITS], in0=beta[:, UNITS : 2 * UNITS], scalar1=1.0)

        acc_o = [
            psum.tile([P, UNITS], F32, tag="bank", bufs=T_BANKS, name="acc_o%d" % m) for m in range(M_TILES)
        ]

        gate_starts = range(0, GROUPS, GATE_CHUNK)
        w_g_tiles = [load_w_gate(2, g0) for g0 in gate_starts]

        def norm_steps(label, rows_by_tile):
            n = len(rows_by_tile[0])
            shape = [P, M_TILES, n]
            neg_mean = keep.tile(shape, F32, name="neg_mean_" + label)
            shift = keep.tile(shape, F32, name="shift_" + label)
            sq_sum = keep.tile(shape, F32, name="sq_sum_" + label)
            root = keep.tile(shape, F32, name="root_" + label)
            rstd = keep.tile(shape, F32, name="rstd_" + label)

            def add_up(m):
                for i, row in enumerate(rows_by_tile[m]):
                    nc.vector.scalar_tensor_tensor(
                        out=row["s"], in0=row["first"], scalar=MEAN_SCALE, in1=row["second"],
                        op0=ALU.mult, op1=ALU.add, accum_out=neg_mean[:, m, i : i + 1],
                    )

            def deviation(m):
                for i, row in enumerate(rows_by_tile[m]):
                    nc.scalar.activation(
                        out=squares[:, m, i, :], in_=row["s"], func=ACT.Square, scale=1.0 / MEAN_SCALE,
                        bias=neg_mean[:, m, i : i + 1], accum_out=sq_sum[:, m, i : i + 1],
                    )
                nc.gpsimd.tensor_tensor(out=root[:, m, :], in0=sq_sum[:, m, :], in1=half[:, 0:n], op=ALU.pow)

            def centre(m):
                nc.vector.tensor_scalar_mul(out=shift[:, m, :], in0=neg_mean[:, m, :], scalar1=MEAN_SCALE)
                for i, row in enumerate(rows_by_tile[m]):
                    nc.vector.scalar_tensor_tensor(
                        out=row["out"], in0=row["s"], scalar=shift[:, m, i : i + 1], in1=row["gamma"],
                        op0=ALU.add, op1=ALU.mult,
                    )

            def finish(m):
                nc.vector.tensor_scalar(
                    out=rstd[:, m, :], in0=root[:, m, :], scalar1=1.0 / math.sqrt(UNITS - 1), scalar2=EPS,
                    op0=ALU.mult, op1=ALU.add,
                )
                nc.vector.reciprocal(out=rstd[:, m, :], in_=rstd[:, m, :])
                for i, row in enumerate(rows_by_tile[m]):
                    nc.vector.scalar_tensor_tensor(
                        out=row["out"], in0=row["out"], scalar=rstd[:, m, i : i + 1], in1=row["beta"],
                        op0=ALU.mult, op1=ALU.add,
                    )

            return add_up, deviation, centre, finish

        def for_tiles(*steps):
            for step in steps:
                for m in range(M_TILES):
                    step(m)

        def gate_row(m, gate, acc):
            return dict(
                first=acc, second=v[:, m, gate_cols(gate)], s=v[:, m, gate_cols(gate)],
                out=gates[:, m, gate_cols(gate)], gamma=gamma[:, gate_cols(gate)], beta=beta[:, gate_cols(gate)],
            )

        gates = stage.tile([P, M_TILES, N], F32, tag="u_sb")
        squares = stage.tile([P, M_TILES, 2, UNITS], F32, tag="u_sb")
        forget_part = keep.tile([P, M_TILES, UNITS], F32)
        in_part = keep.tile([P, M_TILES, UNITS], F32)
        cell = keep.tile([P, M_TILES, UNITS], F32)
        hidden = keep.tile([P, M_TILES, UNITS], F32)

        if_add_up, if_deviation, if_centre, if_finish = norm_steps(
            "if", [[gate_row(m, gate, acc_if[m][:, gate_cols(gate)]) for gate in range(2)] for m in range(M_TILES)]
        )
        g_add_up, g_deviation, g_centre, g_finish = norm_steps(
            "g", [[gate_row(m, 2, acc_g[m][:])] for m in range(M_TILES)]
        )
        cell_add_up, cell_deviation, cell_centre, cell_finish = norm_steps(
            "cell",
            [
                [
                    dict(
                        first=forget_part[:, m, :], second=in_part[:, m, :], s=forget_part[:, m, :],
                        out=cell[:, m, :], gamma=cell_vec[:, 0:UNITS], beta=cell_vec[:, UNITS : 2 * UNITS],
                    )
                ]
                for m in range(M_TILES)
            ],
        )
        o_add_up, o_deviation, o_centre, o_finish = norm_steps(
            "o", [[gate_row(m, 3, acc_o[m][:])] for m in range(M_TILES)]
        )

        def squash(m, cols, func):
            nc.scalar.activation(out=gates[:, m, cols], in_=gates[:, m, cols], func=func)

        def squash_if(m):
            squash(m, slice(0, N_IF), ACT.Sigmoid)

        def squash_g(m):
            squash(m, gate_cols(2), ACT.Tanh)

        def squash_cell(m):
            nc.scalar.activation(out=hidden[:, m, :], in_=cell[:, m, :], func=ACT.Tanh)

        def squash_o(m):
            squash(m, gate_cols(3), ACT.Sigmoid)

        def forget(m):
            nc.vector.tensor_tensor(
                out=forget_part[:, m, :], in0=gates[:, m, gate_cols(1)], in1=hc_sb[:, m, :], op=ALU.mult
            )

        def take_in(m):
            nc.vector.scalar_tensor_tensor(
                out=in_part[:, m, :], in0=gates[:, m, gate_cols(0)], scalar=MEAN_SCALE, in1=gates[:, m, gate_cols(2)],
                op0=ALU.mult, op1=ALU.mult,
            )
            cell_add_up(m)

        def store_hidden(m):
            nc.vector.tensor_tensor(
                out=hidden[:, m, :], in0=hidden[:, m, :], in1=gates[:, m, gate_cols(3)], op=ALU.mult
            )
            nc.sync.dma_start(out=out_0.rearrange("(p m) c -> p m c", m=M_TILES)[:, m, :], in_=hidden[:, m, :])

        for_tiles(if_add_up, if_deviation, if_centre, if_finish, squash_if, forget)

        w_o_tiles = []
        for g0, w_g in zip(gate_starts, w_g_tiles):
            multiply(acc_g, g0, w_g, gate_cols(2))
            w_o_tiles.append(load_w_gate(3, g0))

        for_tiles(g_add_up, g_deviation, g_centre, g_finish, squash_g)
        for_tiles(take_in, cell_deviation, cell_centre, cell_finish, squash_cell)
        nc.sync.dma_start(out=out_1.rearrange("(p m) c -> p m c", m=M_TILES), in_=cell[:])

        for g0, w_o in zip(gate_starts, w_o_tiles):
            multiply(acc_o, g0, w_o, gate_cols(3))
        for_tiles(o_add_up, o_deviation, o_centre, o_finish, squash_o, store_hidden)
